import numpy as np
import ml_dtypes


def mxq(x, axis, fmt="e4m3"):
    dtype, down = {"e4m3": (ml_dtypes.float8_e4m3fn, 7), "e5m2": (ml_dtypes.float8_e5m2, 14)}[fmt]
    v = np.moveaxis(np.asarray(x, np.float32).astype(ml_dtypes.bfloat16).astype(np.float64), axis, -1)
    blocks = v.reshape(v.shape[:-1] + (-1, 32))
    amax = np.abs(blocks).max(-1, keepdims=True)
    byte = np.maximum(np.where(amax > 0, np.frexp(amax)[1] - 1 + 127, 0) - down, 1)
    scale = np.exp2(byte - 127.0)
    codes = (blocks / scale).astype(np.float32).astype(dtype).astype(np.float64)
    return np.moveaxis((codes * scale).reshape(v.shape), -1, axis)


WIDE = False


def mx_kscale(k):
    if not WIDE:
        return np.ones(k)
    levels = np.array([18, -18])
    if k % 512:
        return np.exp2(np.random.permutation(np.resize(levels, k // 32))).repeat(32)
    a = np.empty((k // 512, 16))
    for p in range(k // 512):
        a[p, :8] = np.random.permutation(np.resize(levels, 8))
        for g in range(8):
            far = levels[np.abs(levels - a[p, g]) >= 10]
            a[p, g + 8] = far[np.random.randint(len(far))]
    return np.exp2(a.ravel()).repeat(32)


BF16 = ml_dtypes.bfloat16


def bf(x):
    return np.asarray(x, np.float32).astype(BF16)


def f64(x):
    return np.asarray(x).astype(np.float64)


N, ND, NP, KW = 256, 512, 6, 3
JW = KW - 1
T = N * NP


def tokens(a):
    return a.transpose(2, 0, 1).reshape(T, ND)


def untokens(a):
    return a.reshape(NP, N, ND).transpose(1, 2, 0)


def window_rows(x, d):
    xr = x.reshape(N, ND, NP, JW)
    return np.concatenate([tokens(xr[..., 0]), tokens(xr[..., 1]), tokens(d)], axis=1)


def taps(W):
    return W.transpose(2, 1, 0).reshape(KW * ND, ND)


def pre_activations(x, d_h1, d1, W2, b2, W3, b3):
    a2 = window_rows(f64(x), f64(d_h1)) @ taps(f64(W2)) + f64(b2)
    a2 = untokens(a2)
    a3 = window_rows(f64(x), np.maximum(a2, 0.0)) @ taps(f64(W3)) + f64(b3)
    return a2, untokens(a3) + f64(d1)


def setup_inputs():
    s = mx_kscale(T)
    u = mx_kscale(ND)
    v = mx_kscale(ND)
    st = s.reshape(NP, N).T[:, None, :]
    c = 1.0 / np.sqrt(KW * ND)
    x0 = bf(np.random.standard_normal((N, ND, JW * NP)))
    d_h1_0 = bf(np.maximum(np.random.standard_normal((N, ND, NP)), 0.0))
    d1 = bf(np.random.standard_normal((N, ND, NP)))
    W2_0 = bf(np.random.standard_normal((ND, ND, KW)) * c)
    b2 = bf(np.random.standard_normal(ND) * 0.3)
    W3_0 = bf(np.random.standard_normal((ND, ND, KW)) * c)
    b3 = bf(np.random.standard_normal(ND) * 0.3)
    g = bf(np.random.standard_normal((N, ND, NP)) * np.exp2(np.random.randint(-6, 1, (N, 1, NP))) * 4.0 / st * u[:, None])
    a2, z3 = pre_activations(x0, d_h1_0, d1, W2_0, b2, W3_0, b3)
    return {'x': bf(f64(x0) * np.repeat(st, JW, axis=2)),
            'd_h1': bf(f64(d_h1_0) * st),
            'd1': d1,
            'W2': bf(f64(W2_0) / v[:, None, None]),
            'b2': b2,
            'W3': bf(f64(W3_0) * v[None, :, None] / u[:, None, None]),
            'b3': b3,
            'a2': np.asarray(a2, np.float32),
            'z3': np.asarray(z3, np.float32),
            'grad_out': g}


def reference(x, d_h1, d1, W2, b2, W3, b3, a2, z3, grad_out):
    dz2 = tokens(f64(grad_out)) * (tokens(f64(z3)) > 0.0)
    w3 = f64(W3)[:, :, JW]
    dh = mxq(dz2, 1, 'e5m2') @ mxq(w3, 0, 'e4m3')
    dz1 = dh * (tokens(f64(a2)) > 0.0)
    w2 = f64(W2)[:, :, JW]
    dd = mxq(dz1, 1, 'e5m2') @ mxq(w2, 0, 'e4m3')
    xw = window_rows(f64(x), f64(d_h1))
    dw = mxq(xw, 0, 'e4m3').T @ mxq(dz1, 0, 'e5m2')
    return untokens(dd), dw.reshape(KW, ND, ND).transpose(2, 1, 0)

@@ -1,0 +1,448 @@
+from contextlib import ExitStack
+
+import concourse.mybir as mybir
+from concourse.masks import make_identity
+
+F32 = mybir.dt.float32
+BF16 = mybir.dt.bfloat16
+I32 = mybir.dt.int32
+U8 = mybir.dt.uint8
+E4M3 = mybir.dt.float8_e4m3fn_x4
+E5M2 = mybir.dt.float8_e5m2_x4
+ALU = mybir.AluOpType
+
+P = 128
+N, ND, NP, KW = 256, 512, 6, 3
+T = N * NP
+FLOPS = 2 * (2 * T * ND * ND + T * KW * ND * ND)
+BYTES = 2 * (N * ND * 12 + N * ND * 6 * 2 + 2 * ND * ND) + 4 * (2 * N * ND * 6) + 4 * (N * ND * 6 + ND * ND * 3)
+
+G = 3
+NI = 86
+ISTEP = 85
+LEAD = 8
+XCOLS = 272
+
+
+def tile_dijetresnetblock_pa_v_kernel(tc, x, d_h1, d1, W2, b2, W3, b3, a2, z3, grad_out, out_0, out_1):
+    nc = tc.nc
+
+    x_v = x.rearrange("(p j) (h c) s -> h p j (c s)", j=4, h=2)
+    d_v = d_h1.rearrange("(p j) (h c) s -> h p j (c s)", j=4, h=2)
+    z_v = z3.rearrange("(q e) c s -> e q (c s)", e=2)
+    a_v = a2.rearrange("(q e) c s -> e q (c s)", e=2)
+    g_v = grad_out.rearrange("(q e) c s -> e q (c s)", e=2)
+    w2_v = W2.rearrange("(p t) i k -> p t (i k)", t=4)
+    w3_v = W3.rearrange("(p t) i k -> p t (i k)", t=4)
+    out0_v = out_0.rearrange("(q e) c s -> e q (c s)", e=2)
+    out1_v = out_1.rearrange("o (h c) k -> o h (c k)", h=2)
+
+    with ExitStack() as ctx:
+        sb = ctx.enter_context(tc.tile_pool(name="sb", bufs=1))
+        ps = ctx.enter_context(tc.psum_pool(name="ps", bufs=1))
+
+        ident = sb.tile([P, P], F32, name="ident")
+        make_identity(nc, ident[:])
+
+        xcodes = sb.tile([P, 3, G, 512], I32, name="xcodes", align_bytes=64)
+        xscales = sb.tile([P, 3, G, 512], U8, name="xscales", align_bytes=64)
+        nc.gpsimd.memset(xscales[:].rearrange("p a b c -> p (a b c)").bitcast(I32), 0)
+        tscales = sb.tile([P, 3, G, 256], U8, name="tscales", align_bytes=64)
+        nc.gpsimd.memset(tscales[:].rearrange("p a b c -> p (a b c)").bitcast(I32), 0)
+        codes2 = sb.tile([P, 2, G, 256], I32, name="codes2", align_bytes=64)
+        scales2 = sb.tile([P, 2, G, 256], U8, name="scales2", align_bytes=64)
+        dz1t = sb.tile([P, G, 2, 256, 4], BF16, name="dz1t", align_bytes=64)
+        codes1 = sb.tile([P, G, 2, 256], I32, name="codes1", align_bytes=64)
+        scales1 = sb.tile([P, G, 2, 256], U8, name="scales1", align_bytes=64)
+        tcodes = sb.tile([P, G, 512], I32, name="tcodes", align_bytes=64)
+        tkscales = sb.tile([P, G, 512], U8, name="tkscales", align_bytes=64)
+
+        xraw = {}
+        draw = {}
+        xin = {}
+        tmpc = {}
+        zt = {}
+        gt = {}
+        at = {}
+        wraw = {}
+        wcodes = {}
+        wscales = {}
+        dz2w = {}
+        dz1w = {}
+        stage = {}
+
+        def load_half(w, h, eng):
+            rows = slice(64 * h, 64 * h + 64)
+            eng.dma_start(out=xraw[w][rows], in_=x_v[h][:, :, 12 * ISTEP * w : 12 * (ISTEP * w + NI)])
+            eng.dma_start(out=draw[w][rows], in_=d_v[h][:, :, 6 * ISTEP * w : 6 * (ISTEP * w + NI)])
+
+        def open_x(w):
+            xr = sb.tile([P, 4, NI * 12], BF16, name="xr", tag="xr", bufs=2)
+            dr = sb.tile([P, 4, NI * 6], BF16, name="dr", tag="dr", bufs=2)
+            xraw[w] = xr
+            draw[w] = dr
+            xi = sb.tile([P, NP, XCOLS, 4], BF16, name="xi", tag="xi", bufs=2, align_bytes=64)
+            xin[w] = xi
+            tm = sb.tile([P, G, 256], I32, name="tm", tag="tm", bufs=2, align_bytes=64)
+            tmpc[w] = tm
+
+        def load_zg(e):
+            z = sb.tile([P, 3072], F32, name="z", tag="z", bufs=2)
+            g = sb.tile([P, 3072], BF16, name="g", tag="b6", bufs=4)
+            nc.sync.dma_start(out=z[:], in_=z_v[e])
+            nc.sync.dma_start(out=g[:], in_=g_v[e])
+            zt[e] = z
+            gt[e] = g
+
+        def load_a(e):
+            a = sb.tile([P, 3072], F32, name="a", tag="a", bufs=2)
+            nc.sync.dma_start(out=a[:], in_=a_v[e])
+            at[e] = a
+
+        def load_w(i, view):
+            wr = sb.tile([P, 4, 1536], BF16, name="wr", tag="wr", bufs=1)
+            nc.sync.dma_start(out=wr[:], in_=view)
+            wraw[i] = wr
+
+        def copy_x(w, s, copy):
+            cols = xin[w][:, s, LEAD - w : LEAD - w + 3 * NI, :].rearrange("p (i k) j -> p i k j", k=3)
+            copy(out=cols[:, :, 0:2, :], in_=xraw[w][:].rearrange("p j (i c) -> p i c j", c=12)[:, :, 2 * s : 2 * s + 2, :])
+            copy(out=cols[:, :, 2, :], in_=draw[w][:].rearrange("p j (i c) -> p i c j", c=6)[:, :, s, :])
+
+        def quant_x(w, s):
+            g = s // 2
+            if s % 2 == 0:
+                out = xcodes[:, w, g, 0:256]
+                sc = xscales[:, w, g, 0:256]
+            else:
+                out = tmpc[w][:, g, :]
+                sc = tscales[:, w, g, :]
+            nc.vector.quantize_mx(
+                out=out.bitcast(E4M3),
+                scales=sc,
+                in_=xin[w][:, s, LEAD : LEAD + 256, :].rearrange("p c j -> p (c j)"),
+            )
+
+        def swap_even(w):
+            nc.sync.dma_start(out=xcodes[0:64, w, :, 256:512], in_=xcodes[64:128, w, :, 0:256])
+            nc.sync.dma_start(out=xscales[0:64, w, :, 256:512].bitcast(I32), in_=xscales[64:128, w, :, 0:256].bitcast(I32))
+
+        def swap_odd(w):
+            nc.sync.dma_start(out=xcodes[64:128, w, :, 0:256], in_=tmpc[w][0:64, :, :])
+            nc.sync.dma_start(out=xscales[64:128, w, :, 0:256].bitcast(I32), in_=tscales[0:64, w, :, :].bitcast(I32))
+            nc.vector.tensor_copy(out=xcodes[64:128, w, :, 256:512], in_=tmpc[w][64:128, :, :])
+            nc.vector.tensor_copy(out=xscales[64:128, w, :, 256:512].bitcast(I32), in_=tscales[64:128, w, :, :].bitcast(I32))
+
+        V = nc.vector.tensor_copy
+        A = nc.scalar.copy
+
+        def prep_w(i, copy):
+            win = sb.tile([P, 512, 4], BF16, name="win", tag="win", bufs=1, align_bytes=64)
+            src = wraw[i][:].rearrange("p t (c k) -> p c k t", k=3)[:, :, 2, :]
+            copy(out=win[:], in_=src)
+            wraw[i] = win
+
+        def quant_w(i):
+            wc = sb.tile([P, 512], I32, name="wc", tag="wc", bufs=2, align_bytes=64)
+            ws = sb.tile([P, 512], U8, name="ws", tag="ws", bufs=2, align_bytes=64)
+            nc.vector.quantize_mx(out=wc[:].bitcast(E4M3), scales=ws[:], in_=wraw[i][:].rearrange("p c t -> p (c t)"))
+            wcodes[i] = wc
+            wscales[i] = ws
+
+        def open_dz(store, e):
+            w = sb.tile([P, NP, 512], BF16, name="dz", tag="b6", bufs=4)
+            store[e] = w
+
+        def mask2(e, g):
+            ss = slice(2 * g, 2 * g + 2)
+            zs = zt[e][:].rearrange("q (j s) -> q s j", s=NP)
+            gs = gt[e][:].rearrange("q (j s) -> q s j", s=NP)
+            nc.vector.scalar_tensor_tensor(out=dz2w[e][:, ss, :], in0=zs[:, ss, :], scalar=0.0, in1=gs[:, ss, :], op0=ALU.is_gt, op1=ALU.mult)
+
+        banks = {}
+        tins = {}
+
+        def turn(src, e, g):
+            bank = ps.tile([P, 2, 2, P], F32, name="tp", tag="tp", bufs=3)
+            for half in range(2):
+                words = src[e][:, 2 * g + half, :].bitcast(F32)
+                for u in range(2):
+                    nc.tensor.transpose(bank[:, half, u, :], words[:, u:256:2], ident[:])
+            banks[e, g] = bank
+
+        def out2(e, g, copy):
+            ti = sb.tile([P, 256, 4], BF16, name="ti", tag="ti", bufs=3, align_bytes=64)
+            dst = ti[:].rearrange("p c t -> p (c t)").bitcast(F32).rearrange("p (h q u) -> p h q u", h=2, u=2)
+            copy(out=dst, in_=banks[e, g][:].rearrange("p h u q -> p h q u"))
+            tins[e, g] = ti
+
+        def quant2(e, g):
+            nc.vector.quantize_mx(out=codes2[:, e, g, :].bitcast(E5M2), scales=scales2[:, e, g, :], in_=tins[e, g][:].rearrange("p c t -> p (c t)"))
+
+        accs = {}
+
+        def dh(e, s):
+            g, half = s // 2, s % 2
+            acc = ps.tile([P, 512], F32, name="mm", tag="mm", bufs=5)
+            cols = slice(128 * half, 128 * half + 128)
+            nc.tensor.matmul_mx(out=acc[:], lhsT=codes2[:, e, g, cols].bitcast(E5M2), lhsT_scale=scales2[:, e, g, cols],
+                                rhs=wcodes[3][:].bitcast(E4M3), rhs_scale=wscales[3][:], start=True, stop=True)
+            accs[e, s] = acc
+
+        def mask1(e, s):
+            nc.vector.scalar_tensor_tensor(out=dz1w[e][:, s, :], in0=at[e][:].rearrange("q (o s) -> q s o", s=NP)[:, s, :], scalar=0.0,
+                                           in1=accs[e, s][:], op0=ALU.is_gt, op1=ALU.mult)
+
+        def out1(e, g, copy):
+            dst = dz1t[:, g, e, :, :].rearrange("p c t -> p (c t)").bitcast(F32).rearrange("p (h q u) -> p h q u", h=2, u=2)
+            copy(out=dst, in_=banks[e, g][:].rearrange("p h u q -> p h q u"))
+
+        def quant1(e, g):
+            nc.vector.quantize_mx(out=codes1[:, g, e, :].bitcast(E5M2), scales=scales1[:, g, e, :],
+                                  in_=dz1t[:, g, e, :, :].rearrange("p c t -> p (c t)"))
+
+        kins = {}
+
+        def back(g, u):
+            bank = ps.tile([P, 4, P], F32, name="tp", tag="tp", bufs=3)
+            for t in range(4):
+                words = dz1t[:, g, t % 2, :, :].rearrange("p c t -> p (c t)").bitcast(F32)
+                nc.tensor.transpose(bank[:, t, :], words[:, 2 * (t // 2) + u : 512 : 4], ident[:])
+            banks["k", g, u] = bank
+
+        def outk(g, u, copy):
+            if u == 0:
+                ki = sb.tile([P, 512, 4], BF16, name="ki", tag="ki", bufs=2, align_bytes=64)
+                kins[g] = ki
+            dst = kins[g][:].rearrange("m (p u e) t -> m u p e t", u=2, e=2)
+            copy(out=dst[:, u], in_=banks["k", g, u][:].rearrange("m t p -> m (t p)").bitcast(BF16).rearrange("m (t p e) -> m p e t", t=4, e=2))
+
+        def quantk(g):
+            nc.vector.quantize_mx(out=tcodes[:, g, :].bitcast(E5M2), scales=tkscales[:, g, :], in_=kins[g][:].rearrange("p c t -> p (c t)"))
+
+        def dd(e, s):
+            g, half = s // 2, s % 2
+            acc = ps.tile([P, 512], F32, name="mm", tag="mm", bufs=5)
+            cols = slice(128 * half, 128 * half + 128)
+            nc.tensor.matmul_mx(out=acc[:], lhsT=codes1[:, g, e, cols].bitcast(E5M2), lhsT_scale=scales1[:, g, e, cols],
+                                rhs=wcodes[2][:].bitcast(E4M3), rhs_scale=wscales[2][:], start=True, stop=True)
+            accs["d", e, s] = acc
+
+        def open_stage(e):
+            st = sb.tile([P, NP, 512], F32, name="st", tag="z", bufs=2)
+            stage[e] = st
+            o = sb.tile([P, 3072], F32, name="o0", tag="a", bufs=2)
+            stage["o", e] = o
+
+        def outd(e, s, copy):
+            copy(out=stage[e][:, s, :], in_=accs["d", e, s][:])
+
+        def finish0(e, h, eng):
+            cs = slice(256 * h, 256 * h + 256)
+            ov = stage["o", e][:, 1536 * h : 1536 * h + 1536]
+            nc.vector.tensor_copy(out=ov.rearrange("q (i s) -> q i s", s=NP), in_=stage[e][:, :, cs].rearrange("q s i -> q i s"))
+            eng.dma_start(out=out0_v[e][:, 1536 * h : 1536 * h + 1536], in_=ov)
+
+        def dw(w, ot):
+            acc = ps.tile([P, 512], F32, name="mm", tag="mm", bufs=5)
+            ocols = slice(128 * ot, 128 * ot + 128)
+            for g in range(G):
+                nc.tensor.matmul_mx(out=acc[:], lhsT=tcodes[:, g, ocols].bitcast(E5M2), lhsT_scale=tkscales[:, g, ocols],
+                                    rhs=xcodes[:, w, g, :].bitcast(E4M3), rhs_scale=xscales[:, w, g, :], start=(g == 0), stop=(g == G - 1))
+            accs["w", w, ot] = acc
+
+        def outw(w, ot, copy, eng):
+            ocols = slice(128 * ot, 128 * ot + 128)
+            r = sb.tile([P, 512], F32, name="r1", tag="r1", bufs=4)
+            copy(out=r[:], in_=accs["w", w, ot][:])
+            eng.dma_start(out=out1_v[ocols, :, 256 * w : 256 * w + 256], in_=r[:].rearrange("p (h c) -> p h c", h=2))
+
+        with tc.manual_schedule():
+            warm = sb.tile([P, 1], F32, name="warm")
+            nc.vector.memset(warm[:], 0.0)
+            A(out=warm[:], in_=warm[:])
+            open_x(0)
+            load_half(0, 0, nc.sync)
+            load_half(0, 1, nc.scalar)
+            load_zg(0)
+            load_w(3, w3_v)
+            open_x(1)
+            load_half(1, 0, nc.sync)
+            load_zg(1)
+            load_a(0)
+            copy_x(0, 0, V)
+            copy_x(0, 1, A)
+            copy_x(0, 2, V)
+            quant_x(0, 0)
+            copy_x(0, 3, A)
+            copy_x(0, 4, V)
+            quant_x(0, 2)
+            copy_x(0, 5, A)
+            load_half(1, 1, nc.scalar)
+            open_dz(dz2w, 0)
+            quant_x(0, 1)
+            quant_x(0, 4)
+            swap_even(0)
+            mask2(0, 0)
+            turn(dz2w, 0, 0)
+            out2(0, 0, A)
+            quant_x(0, 3)
+            mask2(0, 1)
+            turn(dz2w, 0, 1)
+            out2(0, 1, A)
+            quant_x(0, 5)
+            swap_odd(0)
+            mask2(0, 2)
+            turn(dz2w, 0, 2)
+            out2(0, 2, A)
+            quant2(0, 0)
+            prep_w(3, A)
+            load_w(2, w2_v)
+            load_a(1)
+            quant2(0, 1)
+            quant2(0, 2)
+            copy_x(1, 0, V)
+            quant_w(3)
+            copy_x(1, 2, V)
+            quant_x(1, 0)
+            copy_x(1, 1, A)
+            copy_x(1, 3, A)
+            copy_x(1, 5, A)
+            copy_x(1, 4, A)
+            quant_x(1, 2)
+            quant_x(1, 1)
+            open_dz(dz2w, 1)
+            open_dz(dz1w, 0)
+            mask2(1, 0)
+            turn(dz2w, 1, 0)
+            mask2(1, 1)
+            turn(dz2w, 1, 1)
+            mask2(1, 2)
+            turn(dz2w, 1, 2)
+            quant_x(1, 3)
+            quant_x(1, 5)
+            quant_x(1, 4)
+            open_x(2)
+            load_half(2, 0, nc.sync)
+            swap_even(1)
+            out2(1, 0, A)
+            out2(1, 1, A)
+            out2(1, 2, A)
+            swap_odd(1)
+            for s in range(4):
+                dh(0, s)
+            mask1(0, 0)
+            quant2(1, 0)
+            mask1(0, 1)
+            turn(dz1w, 0, 0)
+            out1(0, 0, A)
+            dh(0, 4)
+            mask1(0, 2)
+            quant2(1, 1)
+            mask1(0, 3)
+            turn(dz1w, 0, 1)
+            out1(0, 1, A)
+            dh(0, 5)
+            quant1(0, 0)
+            mask1(0, 4)
+            quant2(1, 2)
+            mask1(0, 5)
+            turn(dz1w, 0, 2)
+            out1(0, 2, A)
+            prep_w(2, A)
+            quant1(0, 1)
+            quant1(0, 2)
+            open_stage(0)
+            open_dz(dz1w, 1)
+            for s in range(4):
+                dh(1, s)
+            quant_w(2)
+            load_half(2, 1, nc.scalar)
+            mask1(1, 0)
+            mask1(1, 1)
+            turn(dz1w, 1, 0)
+            dd(0, 0)
+            outd(0, 0, A)
+            out1(1, 0, A)
+            dh(1, 4)
+            mask1(1, 2)
+            quant1(1, 0)
+            mask1(1, 3)
+            turn(dz1w, 1, 1)
+            dd(0, 1)
+            outd(0, 1, A)
+            out1(1, 1, A)
+            dh(1, 5)
+            back(0, 0)
+            back(0, 1)
+            outk(0, 0, A)
+            mask1(1, 4)
+            quant1(1, 1)
+            mask1(1, 5)
+            turn(dz1w, 1, 2)
+            dd(0, 2)
+            outk(0, 1, V)
+            out1(1, 2, A)
+            outd(0, 2, A)
+            back(1, 0)
+            back(1, 1)
+            dd(0, 3)
+            outk(1, 0, A)
+            quant1(1, 2)
+            outk(1, 1, V)
+            quantk(0)
+            outd(0, 3, A)
+            back(2, 0)
+            back(2, 1)
+            dd(0, 4)
+            dd(0, 5)
+            outk(2, 0, A)
+            quantk(1)
+            outk(2, 1, V)
+            outd(0, 4, A)
+            outd(0, 5, A)
+            copy_x(2, 0, V)
+            quantk(2)
+            copy_x(2, 2, V)
+            quant_x(2, 0)
+            copy_x(2, 4, V)
+            quant_x(2, 2)
+            copy_x(2, 1, A)
+            dw(0, 0)
+            dw(0, 1)
+            dw(0, 2)
+            dw(0, 3)
+            finish0(0, 0, nc.gpsimd)
+            quant_x(2, 4)
+            swap_even(2)
+            outw(0, 0, A, nc.scalar)
+            copy_x(2, 3, A)
+            copy_x(2, 5, V)
+            quant_x(2, 1)
+            finish0(0, 1, nc.gpsimd)
+            outw(0, 1, A, nc.scalar)
+            quant_x(2, 5)
+            quant_x(2, 3)
+            swap_odd(2)
+            open_stage(1)
+            dd(1, 0)
+            dd(1, 1)
+            dd(1, 2)
+            outw(0, 2, V, nc.gpsimd)
+            outw(0, 3, A, nc.scalar)
+            dd(1, 3)
+            dd(1, 4)
+            dd(1, 5)
+            for s in range(6):
+                outd(1, s, V if s == 1 or s == 4 else A)
+            for ot in range(4):
+                dw(1, ot)
+            finish0(1, 0, nc.gpsimd)
+            outw(1, 0, A, nc.scalar)
+            finish0(1, 1, nc.gpsimd)
+            outw(1, 1, A, nc.scalar)
+            outw(1, 2, V, nc.gpsimd)
+            outw(1, 3, A, nc.scalar)
+            for ot in range(4):
+                dw(2, ot)
+                outw(2, ot, A if ot % 2 == 0 else V, nc.scalar if ot % 2 == 0 else nc.sync)

@@ -18,10 +18,7 @@ FLOPS = 2 * (2 * T * ND * ND + T * KW * ND * ND)
 BYTES = 2 * (N * ND * 12 + N * ND * 6 * 2 + 2 * ND * ND) + 4 * (2 * N * ND * 6) + 4 * (N * ND * 6 + ND * ND * 3)
 
 G = 3
-NI = 86
-ISTEP = 85
-LEAD = 8
-XCOLS = 272
+NI = 85
 
 
 def tile_dijetresnetblock_pa_v_kernel(tc, x, d_h1, d1, W2, b2, W3, b3, a2, z3, grad_out, out_0, out_1):
@@ -36,6 +33,8 @@ def tile_dijetresnetblock_pa_v_kernel(tc, x, d_h1, d1, W2, b2, W3, b3, a2, z3, g
     w3_v = W3.rearrange("(p t) i k -> p t (i k)", t=4)
     out0_v = out_0.rearrange("(q e) c s -> e q (c s)", e=2)
     out1_v = out_1.rearrange("o (h c) k -> o h (c k)", h=2)
+    V = nc.vector.tensor_copy
+    A = nc.scalar.copy
 
     with ExitStack() as ctx:
         sb = ctx.enter_context(tc.tile_pool(name="sb", bufs=1))
@@ -56,43 +55,60 @@ def tile_dijetresnetblock_pa_v_kernel(tc, x, d_h1, d1, W2, b2, W3, b3, a2, z3, g
         scales1 = sb.tile([P, G, 2, 256], U8, name="scales1", align_bytes=64)
         tcodes = sb.tile([P, G, 512], I32, name="tcodes", align_bytes=64)
         tkscales = sb.tile([P, G, 512], U8, name="tkscales", align_bytes=64)
+        draw = sb.tile([P, 4, 256 * 6], BF16, name="draw")
+        xlast = sb.tile([P, 4, 12], BF16, name="xlast")
 
         xraw = {}
-        draw = {}
         xin = {}
         tmpc = {}
         zt = {}
         gt = {}
         at = {}
         wraw = {}
+        wins = {}
         wcodes = {}
         wscales = {}
         dz2w = {}
         dz1w = {}
+        m1 = {}
         stage = {}
-
-        def load_half(w, h, eng):
-            rows = slice(64 * h, 64 * h + 64)
-            eng.dma_start(out=xraw[w][rows], in_=x_v[h][:, :, 12 * ISTEP * w : 12 * (ISTEP * w + NI)])
-            eng.dma_start(out=draw[w][rows], in_=d_v[h][:, :, 6 * ISTEP * w : 6 * (ISTEP * w + NI)])
+        rows1 = {}
+        banks = {}
+        tins = {}
+        accs = {}
+        kins = {}
 
         def open_x(w):
             xr = sb.tile([P, 4, NI * 12], BF16, name="xr", tag="xr", bufs=2)
-            dr = sb.tile([P, 4, NI * 6], BF16, name="dr", tag="dr", bufs=2)
             xraw[w] = xr
-            draw[w] = dr
-            xi = sb.tile([P, NP, XCOLS, 4], BF16, name="xi", tag="xi", bufs=2, align_bytes=64)
+
+        def open_xi(w):
+            xi = sb.tile([P, NP, 256, 4], BF16, name="xi", tag="xi", bufs=2, align_bytes=64)
             xin[w] = xi
+
+        def open_tmp(w):
             tm = sb.tile([P, G, 256], I32, name="tm", tag="tm", bufs=2, align_bytes=64)
             tmpc[w] = tm
 
-        def load_zg(e):
+        def load_x(w, h, eng):
+            eng.dma_start(out=xraw[w][64 * h : 64 * h + 64], in_=x_v[h][:, :, 12 * NI * w : 12 * NI * (w + 1)])
+
+        def load_last(h, eng):
+            eng.dma_start(out=xlast[64 * h : 64 * h + 64], in_=x_v[h][:, :, 12 * 255 : 12 * 256])
+
+        def load_d(h, eng):
+            eng.dma_start(out=draw[64 * h : 64 * h + 64], in_=d_v[h])
+
+        def open_zg(e):
             z = sb.tile([P, 3072], F32, name="z", tag="z", bufs=2)
-            g = sb.tile([P, 3072], BF16, name="g", tag="b6", bufs=4)
-            nc.sync.dma_start(out=z[:], in_=z_v[e])
-            nc.sync.dma_start(out=g[:], in_=g_v[e])
+            g = sb.tile([P, 3072], BF16, name="g", tag="b6", bufs=5)
             zt[e] = z
             gt[e] = g
+
+        def load_zg(e, h):
+            c = slice(1536 * h, 1536 * h + 1536)
+            nc.sync.dma_start(out=zt[e][:, c], in_=z_v[e][:, c])
+            nc.sync.dma_start(out=gt[e][:, c], in_=g_v[e][:, c])
 
         def load_a(e):
             a = sb.tile([P, 3072], F32, name="a", tag="a", bufs=2)
@@ -105,9 +121,20 @@ def tile_dijetresnetblock_pa_v_kernel(tc, x, d_h1, d1, W2, b2, W3, b3, a2, z3, g
             wraw[i] = wr
 
         def copy_x(w, s, copy):
-            cols = xin[w][:, s, LEAD - w : LEAD - w + 3 * NI, :].rearrange("p (i k) j -> p i k j", k=3)
-            copy(out=cols[:, :, 0:2, :], in_=xraw[w][:].rearrange("p j (i c) -> p i c j", c=12)[:, :, 2 * s : 2 * s + 2, :])
-            copy(out=cols[:, :, 2, :], in_=draw[w][:].rearrange("p j (i c) -> p i c j", c=6)[:, :, s, :])
+            copy(out=xin[w][:, s, 0 : 2 * NI, :].rearrange("p (k i) j -> p i k j", k=2),
+                 in_=xraw[w][:].rearrange("p j (i c) -> p i c j", c=12)[:, :, 2 * s : 2 * s + 2, :])
+
+        def copy_d(w, g, copy):
+            ss = slice(2 * g, 2 * g + 2)
+            copy(out=xin[w][:, ss, 2 * NI : 3 * NI, :].rearrange("p s i j -> p i s j"),
+                 in_=draw[:].rearrange("p j (i c) -> p i c j", c=6)[:, NI * w : NI * (w + 1), ss, :])
+
+        def copy_last(w, copy):
+            if w < 2:
+                src = xlast[:].rearrange("p j (s k) -> p s k j", k=2)[:, :, w, :]
+            else:
+                src = draw[:].rearrange("p j (i c) -> p i c j", c=6)[:, 255, :, :]
+            copy(out=xin[w][:, :, 255, :], in_=src)
 
         def quant_x(w, s):
             g = s // 2
@@ -117,11 +144,7 @@ def tile_dijetresnetblock_pa_v_kernel(tc, x, d_h1, d1, W2, b2, W3, b3, a2, z3, g
             else:
                 out = tmpc[w][:, g, :]
                 sc = tscales[:, w, g, :]
-            nc.vector.quantize_mx(
-                out=out.bitcast(E4M3),
-                scales=sc,
-                in_=xin[w][:, s, LEAD : LEAD + 256, :].rearrange("p c j -> p (c j)"),
-            )
+            nc.vector.quantize_mx(out=out.bitcast(E4M3), scales=sc, in_=xin[w][:, s, :, :].rearrange("p c j -> p (c j)"))
 
         def swap_even(w):
             nc.sync.dma_start(out=xcodes[0:64, w, :, 256:512], in_=xcodes[64:128, w, :, 0:256])
@@ -130,37 +153,44 @@ def tile_dijetresnetblock_pa_v_kernel(tc, x, d_h1, d1, W2, b2, W3, b3, a2, z3, g
         def swap_odd(w):
             nc.sync.dma_start(out=xcodes[64:128, w, :, 0:256], in_=tmpc[w][0:64, :, :])
             nc.sync.dma_start(out=xscales[64:128, w, :, 0:256].bitcast(I32), in_=tscales[0:64, w, :, :].bitcast(I32))
-            nc.vector.tensor_copy(out=xcodes[64:128, w, :, 256:512], in_=tmpc[w][64:128, :, :])
-            nc.vector.tensor_copy(out=xscales[64:128, w, :, 256:512].bitcast(I32), in_=tscales[64:128, w, :, :].bitcast(I32))
 
-        V = nc.vector.tensor_copy
-        A = nc.scalar.copy
+        def keep_odd(w):
+            nc.sync.dma_start(out=xcodes[64:128, w, :, 256:512], in_=tmpc[w][64:128, :, :])
+            nc.sync.dma_start(out=xscales[64:128, w, :, 256:512].bitcast(I32), in_=tscales[64:128, w, :, :].bitcast(I32))
 
-        def prep_w(i, copy):
+        def open_w(i):
             win = sb.tile([P, 512, 4], BF16, name="win", tag="win", bufs=1, align_bytes=64)
-            src = wraw[i][:].rearrange("p t (c k) -> p c k t", k=3)[:, :, 2, :]
-            copy(out=win[:], in_=src)
-            wraw[i] = win
+            wins[i] = win
+
+        def prep_w(i, h, copy):
+            c = slice(256 * h, 256 * h + 256)
+            copy(out=wins[i][:, c, :], in_=wraw[i][:].rearrange("p t (c k) -> p c k t", k=3)[:, c, 2, :])
 
         def quant_w(i):
             wc = sb.tile([P, 512], I32, name="wc", tag="wc", bufs=2, align_bytes=64)
             ws = sb.tile([P, 512], U8, name="ws", tag="ws", bufs=2, align_bytes=64)
-            nc.vector.quantize_mx(out=wc[:].bitcast(E4M3), scales=ws[:], in_=wraw[i][:].rearrange("p c t -> p (c t)"))
+            nc.vector.quantize_mx(out=wc[:].bitcast(E4M3), scales=ws[:], in_=wins[i][:].rearrange("p c t -> p (c t)"))
             wcodes[i] = wc
             wscales[i] = ws
 
         def open_dz(store, e):
-            w = sb.tile([P, NP, 512], BF16, name="dz", tag="b6", bufs=4)
+            w = sb.tile([P, NP, 512], BF16, name="dz", tag="b6", bufs=5)
             store[e] = w
 
-        def mask2(e, g):
+        def mask2(e, g, h):
             ss = slice(2 * g, 2 * g + 2)
-            zs = zt[e][:].rearrange("q (j s) -> q s j", s=NP)
-            gs = gt[e][:].rearrange("q (j s) -> q s j", s=NP)
-            nc.vector.scalar_tensor_tensor(out=dz2w[e][:, ss, :], in0=zs[:, ss, :], scalar=0.0, in1=gs[:, ss, :], op0=ALU.is_gt, op1=ALU.mult)
+            c = slice(256 * h, 256 * h + 256)
+            nc.vector.scalar_tensor_tensor(out=dz2w[e][:, ss, c].rearrange("q s j -> q j s"), in0=zt[e][:].rearrange("q (j s) -> q j s", s=NP)[:, c, ss],
+                                           scalar=0.0, in1=gt[e][:].rearrange("q (j s) -> q j s", s=NP)[:, c, ss], op0=ALU.is_gt, op1=ALU.mult)
 
-        banks = {}
-        tins = {}
+        def sign1(e, g, act):
+            ss = slice(2 * g, 2 * g + 2)
+            dst = m1[e][:, ss, :].rearrange("q s o -> q o s")
+            src = at[e][:].rearrange("q (o s) -> q o s", s=NP)[:, :, ss]
+            if act:
+                nc.scalar.activation(out=dst, in_=src, func=mybir.ActivationFunctionType.Sign)
+            else:
+                nc.vector.tensor_scalar(out=dst, in0=src, scalar1=0.0, scalar2=None, op0=ALU.is_gt)
 
         def turn(src, e, g):
             bank = ps.tile([P, 2, 2, P], F32, name="tp", tag="tp", bufs=3)
@@ -179,8 +209,6 @@ def tile_dijetresnetblock_pa_v_kernel(tc, x, d_h1, d1, W2, b2, W3, b3, a2, z3, g
         def quant2(e, g):
             nc.vector.quantize_mx(out=codes2[:, e, g, :].bitcast(E5M2), scales=scales2[:, e, g, :], in_=tins[e, g][:].rearrange("p c t -> p (c t)"))
 
-        accs = {}
-
         def dh(e, s):
             g, half = s // 2, s % 2
             acc = ps.tile([P, 512], F32, name="mm", tag="mm", bufs=5)
@@ -190,8 +218,7 @@ def tile_dijetresnetblock_pa_v_kernel(tc, x, d_h1, d1, W2, b2, W3, b3, a2, z3, g
             accs[e, s] = acc
 
         def mask1(e, s):
-            nc.vector.scalar_tensor_tensor(out=dz1w[e][:, s, :], in0=at[e][:].rearrange("q (o s) -> q s o", s=NP)[:, s, :], scalar=0.0,
-                                           in1=accs[e, s][:], op0=ALU.is_gt, op1=ALU.mult)
+            nc.vector.scalar_tensor_tensor(out=dz1w[e][:, s, :], in0=m1[e][:, s, :], scalar=0.0, in1=accs[e, s][:], op0=ALU.max, op1=ALU.mult)
 
         def out1(e, g, copy):
             dst = dz1t[:, g, e, :, :].rearrange("p c t -> p (c t)").bitcast(F32).rearrange("p (h q u) -> p h q u", h=2, u=2)
@@ -200,8 +227,6 @@ def tile_dijetresnetblock_pa_v_kernel(tc, x, d_h1, d1, W2, b2, W3, b3, a2, z3, g
         def quant1(e, g):
             nc.vector.quantize_mx(out=codes1[:, g, e, :].bitcast(E5M2), scales=scales1[:, g, e, :],
                                   in_=dz1t[:, g, e, :, :].rearrange("p c t -> p (c t)"))
-
-        kins = {}
 
         def back(g, u):
             bank = ps.tile([P, 4, P], F32, name="tp", tag="tp", bufs=3)
@@ -231,17 +256,23 @@ def tile_dijetresnetblock_pa_v_kernel(tc, x, d_h1, d1, W2, b2, W3, b3, a2, z3, g
         def open_stage(e):
             st = sb.tile([P, NP, 512], F32, name="st", tag="z", bufs=2)
             stage[e] = st
-            o = sb.tile([P, 3072], F32, name="o0", tag="a", bufs=2)
-            stage["o", e] = o
 
         def outd(e, s, copy):
             copy(out=stage[e][:, s, :], in_=accs["d", e, s][:])
 
-        def finish0(e, h, eng):
-            cs = slice(256 * h, 256 * h + 256)
-            ov = stage["o", e][:, 1536 * h : 1536 * h + 1536]
-            nc.vector.tensor_copy(out=ov.rearrange("q (i s) -> q i s", s=NP), in_=stage[e][:, :, cs].rearrange("q s i -> q i s"))
-            eng.dma_start(out=out0_v[e][:, 1536 * h : 1536 * h + 1536], in_=ov)
+        def finish0(e, h):
+            o = sb.tile([P, 1536], F32, name="o0", tag="b6", bufs=5)
+            nc.vector.tensor_copy(out=o[:].rearrange("q (i s) -> q i s", s=NP), in_=stage[e][:, :, 256 * h : 256 * h + 256].rearrange("q s i -> q i s"))
+            stage["o", e, h] = o
+
+        def store0(e, h):
+            nc.sync.dma_start(out=out0_v[e][:, 1536 * h : 1536 * h + 1536], in_=stage["o", e, h][:])
+
+        def open_rows():
+            for i in range(2):
+                r = sb.tile([P, 2, 2, 768], F32, name="r1", tag="a", bufs=2)
+                rows1[2 * i] = r[:, 0]
+                rows1[2 * i + 1] = r[:, 1]
 
         def dw(w, ot):
             acc = ps.tile([P, 512], F32, name="mm", tag="mm", bufs=5)
@@ -251,198 +282,281 @@ def tile_dijetresnetblock_pa_v_kernel(tc, x, d_h1, d1, W2, b2, W3, b3, a2, z3, g
                                     rhs=xcodes[:, w, g, :].bitcast(E4M3), rhs_scale=xscales[:, w, g, :], start=(g == 0), stop=(g == G - 1))
             accs["w", w, ot] = acc
 
-        def outw(w, ot, copy, eng):
-            ocols = slice(128 * ot, 128 * ot + 128)
-            r = sb.tile([P, 512], F32, name="r1", tag="r1", bufs=4)
-            copy(out=r[:], in_=accs["w", w, ot][:])
-            eng.dma_start(out=out1_v[ocols, :, 256 * w : 256 * w + 256], in_=r[:].rearrange("p (h c) -> p h c", h=2))
+        def outw(w, ot, copy):
+            r = rows1[ot]
+            bank = accs["w", w, ot][:].rearrange("m (h c) -> m h c", h=2)
+            copy(out=r[:, :, 255 * w : 255 * w + 255].rearrange("m h (i k) -> m h i k", k=3), in_=bank[:, :, 0:255].rearrange("m h (k i) -> m h i k", k=3))
+            copy(out=r[:, :, 765 + w], in_=bank[:, :, 255])
+
+        def storew(ot, lo, hi):
+            r = rows1[ot]
+            nc.sync.dma_start(out=out1_v[128 * ot : 128 * ot + 128, :, lo:hi], in_=r[:, :, lo:hi])
 
         with tc.manual_schedule():
             warm = sb.tile([P, 1], F32, name="warm")
             nc.vector.memset(warm[:], 0.0)
             A(out=warm[:], in_=warm[:])
-            open_x(0)
-            load_half(0, 0, nc.sync)
-            load_half(0, 1, nc.scalar)
-            load_zg(0)
+            open_zg(0)
+            load_zg(0, 1)
+            load_zg(0, 0)
             load_w(3, w3_v)
-            open_x(1)
-            load_half(1, 0, nc.sync)
-            load_zg(1)
-            load_a(0)
-            copy_x(0, 0, V)
-            copy_x(0, 1, A)
-            copy_x(0, 2, V)
-            quant_x(0, 0)
-            copy_x(0, 3, A)
-            copy_x(0, 4, V)
-            quant_x(0, 2)
-            copy_x(0, 5, A)
-            load_half(1, 1, nc.scalar)
             open_dz(dz2w, 0)
-            quant_x(0, 1)
-            quant_x(0, 4)
-            swap_even(0)
-            mask2(0, 0)
-            turn(dz2w, 0, 0)
-            out2(0, 0, A)
-            quant_x(0, 3)
-            mask2(0, 1)
+            mask2(0, 2, 1)
+            mask2(0, 0, 1)
+            mask2(0, 1, 1)
+            mask2(0, 1, 0)
+            load_a(0)
+            mask2(0, 0, 0)
             turn(dz2w, 0, 1)
-            out2(0, 1, A)
-            quant_x(0, 5)
-            swap_odd(0)
-            mask2(0, 2)
+            mask2(0, 2, 0)
+            turn(dz2w, 0, 0)
+            out2(0, 1, V)
             turn(dz2w, 0, 2)
-            out2(0, 2, A)
-            quant2(0, 0)
-            prep_w(3, A)
-            load_w(2, w2_v)
-            load_a(1)
             quant2(0, 1)
-            quant2(0, 2)
-            copy_x(1, 0, V)
+            out2(0, 0, A)
+            open_w(3)
+            prep_w(3, 0, V)
+            prep_w(3, 1, A)
+            open_zg(1)
+            load_zg(1, 1)
+            quant2(0, 0)
+            out2(0, 2, V)
             quant_w(3)
-            copy_x(1, 2, V)
-            quant_x(1, 0)
-            copy_x(1, 1, A)
-            copy_x(1, 3, A)
-            copy_x(1, 5, A)
-            copy_x(1, 4, A)
-            quant_x(1, 2)
-            quant_x(1, 1)
-            open_dz(dz2w, 1)
+            quant2(0, 2)
+            dh(0, 2)
+            dh(0, 1)
+            load_d(0, nc.sync)
+            load_d(1, nc.scalar)
+            dh(0, 3)
+            open_dz(m1, 0)
+            sign1(0, 1, False)
+            dh(0, 0)
+            dh(0, 5)
+            sign1(0, 0, False)
+            sign1(0, 2, False)
             open_dz(dz1w, 0)
-            mask2(1, 0)
-            turn(dz2w, 1, 0)
-            mask2(1, 1)
+            mask1(0, 2)
+            mask1(0, 1)
+            dh(0, 4)
+            load_zg(1, 0)
+            mask1(0, 5)
+            mask1(0, 4)
+            open_dz(dz2w, 1)
+            mask2(1, 2, 1)
+            turn(dz1w, 0, 2)
+            mask1(0, 3)
+            mask1(0, 0)
+            out1(0, 2, A)
+            turn(dz1w, 0, 1)
+            load_a(1)
+            mask2(1, 0, 1)
+            turn(dz1w, 0, 0)
+            mask2(1, 1, 1)
+            out1(0, 1, A)
+            open_xi(0)
+            copy_d(0, 2, V)
+            copy_d(0, 0, A)
+            copy_d(0, 1, V)
+            quant1(0, 2)
+            out1(0, 0, A)
+            open_xi(1)
+            copy_d(1, 2, A)
+            quant1(0, 0)
+            quant1(0, 1)
+            open_x(0)
+            load_x(0, 0, nc.sync)
+            load_x(0, 1, nc.scalar)
+            load_last(0, nc.sync)
+            load_last(1, nc.scalar)
+            mask2(1, 1, 0)
+            copy_d(1, 0, A)
+            mask2(1, 0, 0)
             turn(dz2w, 1, 1)
-            mask2(1, 2)
+            copy_d(1, 1, A)
+            mask2(1, 2, 0)
+            turn(dz2w, 1, 0)
+            out2(1, 1, V)
+            open_x(1)
+            load_x(1, 0, nc.sync)
+            load_x(1, 1, nc.scalar)
             turn(dz2w, 1, 2)
+            quant2(1, 1)
+            out2(1, 0, A)
+            open_dz(m1, 1)
+            sign1(1, 1, False)
+            sign1(1, 0, True)
+            dh(1, 2)
+            quant2(1, 0)
+            dh(1, 3)
+            open_dz(dz1w, 1)
+            mask1(1, 2)
+            dh(1, 0)
+            out2(1, 2, A)
+            load_w(2, w2_v)
+            mask1(1, 3)
+            dh(1, 1)
+            sign1(1, 2, True)
+            mask1(1, 0)
+            turn(dz1w, 1, 1)
+            mask1(1, 1)
+            copy_x(0, 2, A)
+            copy_x(0, 3, V)
+            turn(dz1w, 1, 0)
+            quant2(1, 2)
+            out1(1, 1, A)
+            copy_x(0, 1, V)
+            dh(1, 4)
+            copy_last(1, A)
+            copy_x(0, 4, A)
+            dh(1, 5)
+            copy_x(1, 2, V)
+            mask1(1, 5)
+            out1(1, 0, A)
+            mask1(1, 4)
+            copy_x(1, 5, A)
+            back(0, 0)
+            copy_x(1, 0, V)
+            copy_last(0, A)
+            quant_x(1, 2)
+            copy_x(1, 1, A)
+            copy_x(1, 3, V)
+            turn(dz1w, 1, 2)
+            copy_x(1, 4, V)
+            outk(0, 0, A)
+            open_tmp(1)
             quant_x(1, 3)
+            back(0, 1)
+            quant_x(1, 1)
             quant_x(1, 5)
             quant_x(1, 4)
-            open_x(2)
-            load_half(2, 0, nc.sync)
-            swap_even(1)
-            out2(1, 0, A)
-            out2(1, 1, A)
-            out2(1, 2, A)
-            swap_odd(1)
-            for s in range(4):
-                dh(0, s)
-            mask1(0, 0)
-            quant2(1, 0)
-            mask1(0, 1)
-            turn(dz1w, 0, 0)
-            out1(0, 0, A)
-            dh(0, 4)
-            mask1(0, 2)
-            quant2(1, 1)
-            mask1(0, 3)
-            turn(dz1w, 0, 1)
-            out1(0, 1, A)
-            dh(0, 5)
-            quant1(0, 0)
-            mask1(0, 4)
-            quant2(1, 2)
-            mask1(0, 5)
-            turn(dz1w, 0, 2)
-            out1(0, 2, A)
-            prep_w(2, A)
-            quant1(0, 1)
-            quant1(0, 2)
-            open_stage(0)
-            open_dz(dz1w, 1)
-            for s in range(4):
-                dh(1, s)
-            quant_w(2)
-            load_half(2, 1, nc.scalar)
-            mask1(1, 0)
-            mask1(1, 1)
-            turn(dz1w, 1, 0)
-            dd(0, 0)
-            outd(0, 0, A)
-            out1(1, 0, A)
-            dh(1, 4)
-            mask1(1, 2)
-            quant1(1, 0)
-            mask1(1, 3)
-            turn(dz1w, 1, 1)
-            dd(0, 1)
-            outd(0, 1, A)
-            out1(1, 1, A)
-            dh(1, 5)
-            back(0, 0)
-            back(0, 1)
-            outk(0, 0, A)
-            mask1(1, 4)
-            quant1(1, 1)
-            mask1(1, 5)
-            turn(dz1w, 1, 2)
-            dd(0, 2)
-            outk(0, 1, V)
             out1(1, 2, A)
-            outd(0, 2, A)
+            keep_odd(1)
+            quant_x(1, 0)
             back(1, 0)
+            outk(0, 1, A)
+            copy_x(0, 0, V)
+            swap_even(1)
+            copy_x(0, 5, V)
+            open_x(2)
+            load_x(2, 0, nc.sync)
+            load_x(2, 1, nc.scalar)
+            open_w(2)
+            prep_w(2, 1, V)
             back(1, 1)
-            dd(0, 3)
             outk(1, 0, A)
-            quant1(1, 2)
-            outk(1, 1, V)
-            quantk(0)
-            outd(0, 3, A)
+            open_tmp(0)
+            quant_x(0, 5)
+            quant_x(0, 3)
+            quant_x(0, 0)
+            prep_w(2, 0, A)
+            quant_x(0, 2)
             back(2, 0)
+            quantk(0)
+            swap_odd(1)
+            quant_x(0, 4)
+            outk(1, 1, A)
+            quant_x(0, 1)
             back(2, 1)
-            dd(0, 4)
-            dd(0, 5)
+            swap_even(0)
+            quant_w(2)
+            keep_odd(0)
+            open_xi(2)
+            copy_d(2, 0, V)
             outk(2, 0, A)
+            dd(0, 1)
+            copy_d(2, 2, V)
+            dd(0, 4)
             quantk(1)
-            outk(2, 1, V)
-            outd(0, 4, A)
-            outd(0, 5, A)
-            copy_x(2, 0, V)
-            quantk(2)
+            dd(0, 3)
+            copy_last(2, A)
+            copy_d(2, 1, V)
+            outk(2, 1, A)
+            dd(0, 0)
             copy_x(2, 2, V)
+            swap_odd(0)
+            dd(0, 5)
+            copy_x(2, 0, V)
+            open_stage(0)
+            outd(0, 1, A)
+            quantk(2)
+            outd(0, 4, A)
+            dd(0, 2)
             quant_x(2, 0)
-            copy_x(2, 4, V)
             quant_x(2, 2)
-            copy_x(2, 1, A)
-            dw(0, 0)
-            dw(0, 1)
-            dw(0, 2)
-            dw(0, 3)
-            finish0(0, 0, nc.gpsimd)
+            outd(0, 0, A)
+            dw(1, 2)
+            copy_x(2, 4, V)
+            outd(0, 3, A)
+            copy_x(2, 1, V)
             quant_x(2, 4)
-            swap_even(2)
-            outw(0, 0, A, nc.scalar)
-            copy_x(2, 3, A)
-            copy_x(2, 5, V)
+            outd(0, 5, A)
+            open_tmp(2)
             quant_x(2, 1)
-            finish0(0, 1, nc.gpsimd)
-            outw(0, 1, A, nc.scalar)
-            quant_x(2, 5)
+            dw(1, 1)
+            swap_even(2)
+            open_rows()
+            outw(1, 2, V)
+            outd(0, 2, A)
+            copy_x(2, 3, V)
+            dw(1, 0)
+            outw(1, 1, A)
+            copy_x(2, 5, V)
             quant_x(2, 3)
+            storew(2, 256, 504)
+            dw(0, 3)
+            quant_x(2, 5)
+            outw(1, 0, A)
+            storew(1, 256, 504)
+            finish0(0, 1)
+            keep_odd(2)
+            dw(0, 2)
             swap_odd(2)
-            open_stage(1)
-            dd(1, 0)
-            dd(1, 1)
-            dd(1, 2)
-            outw(0, 2, V, nc.gpsimd)
-            outw(0, 3, A, nc.scalar)
-            dd(1, 3)
+            outw(0, 3, A)
+            storew(0, 256, 504)
+            dw(0, 0)
+            storew(3, 0, 248)
+            outw(0, 2, A)
+            quant1(1, 1)
+            quant1(1, 2)
+            quant1(1, 0)
+            dw(0, 1)
+            outw(0, 0, A)
+            finish0(0, 0)
+            store0(0, 1)
             dd(1, 4)
+            outw(0, 1, A)
+            dd(1, 0)
+            open_stage(1)
+            outd(1, 4, V)
+            dd(1, 2)
+            storew(1, 0, 256)
+            dd(1, 1)
+            outd(1, 0, V)
+            outd(1, 2, A)
+            store0(0, 0)
+            dd(1, 3)
+            outd(1, 1, V)
             dd(1, 5)
-            for s in range(6):
-                outd(1, s, V if s == 1 or s == 4 else A)
-            for ot in range(4):
-                dw(1, ot)
-            finish0(1, 0, nc.gpsimd)
-            outw(1, 0, A, nc.scalar)
-            finish0(1, 1, nc.gpsimd)
-            outw(1, 1, A, nc.scalar)
-            outw(1, 2, V, nc.gpsimd)
-            outw(1, 3, A, nc.scalar)
-            for ot in range(4):
-                dw(2, ot)
-                outw(2, ot, A if ot % 2 == 0 else V, nc.scalar if ot % 2 == 0 else nc.sync)
+            outd(1, 3, A)
+            dw(2, 1)
+            outd(1, 5, V)
+            storew(2, 0, 256)
+            finish0(1, 0)
+            dw(2, 0)
+            storew(0, 0, 256)
+            outw(2, 1, A)
+            storew(1, 504, 768)
+            dw(2, 2)
+            outw(2, 0, A)
+            finish0(1, 1)
+            store0(1, 0)
+            dw(2, 3)
+            outw(2, 2, A)
+            dw(1, 3)
+            outw(2, 3, A)
+            store0(1, 1)
+            outw(1, 3, V)
+            storew(2, 504, 768)
+            storew(0, 504, 768)
+            storew(3, 248, 504)
+            storew(3, 504, 768)

@@ -48,13 +48,12 @@ def tile_dijetresnetblock_pa_v_kernel(tc, x, d_h1, d1, W2, b2, W3, b3, a2, z3, g
         nc.gpsimd.memset(xscales[:].rearrange("p a b c -> p (a b c)").bitcast(I32), 0)
         tscales = sb.tile([P, 3, G, 256], U8, name="tscales", align_bytes=64)
         nc.gpsimd.memset(tscales[:].rearrange("p a b c -> p (a b c)").bitcast(I32), 0)
-        codes2 = sb.tile([P, 2, G, 256], I32, name="codes2", align_bytes=64)
-        scales2 = sb.tile([P, 2, G, 256], U8, name="scales2", align_bytes=64)
+        codes2 = sb.tile([P, 2, G, 256], I32, name="codes2", tag="c6", align_bytes=64)
+        scales2 = sb.tile([P, 2, G, 256], U8, name="scales2", tag="s6", align_bytes=64)
         dz1t = sb.tile([P, G, 2, 256, 4], BF16, name="dz1t", align_bytes=64)
         codes1 = sb.tile([P, G, 2, 256], I32, name="codes1", align_bytes=64)
         scales1 = sb.tile([P, G, 2, 256], U8, name="scales1", align_bytes=64)
-        tcodes = sb.tile([P, G, 512], I32, name="tcodes", align_bytes=64)
-        tkscales = sb.tile([P, G, 512], U8, name="tkscales", align_bytes=64)
+        tok = {}
         draw = sb.tile([P, 4, 256 * 6], BF16, name="draw")
         xlast = sb.tile([P, 4, 12], BF16, name="xlast")
 
@@ -79,7 +78,7 @@ def tile_dijetresnetblock_pa_v_kernel(tc, x, d_h1, d1, W2, b2, W3, b3, a2, z3, g
         kins = {}
 
         def open_x(w):
-            xr = sb.tile([P, 4, NI * 12], BF16, name="xr", tag="xr", bufs=2)
+            xr = sb.tile([P, 4, NI * 12], BF16, name="xr", tag="xr", bufs=3)
             xraw[w] = xr
 
         def open_xi(w):
@@ -105,24 +104,29 @@ def tile_dijetresnetblock_pa_v_kernel(tc, x, d_h1, d1, W2, b2, W3, b3, a2, z3, g
             zt[e] = z
             gt[e] = g
 
-        def load_zg(e, h):
+        def load_zg(e, h, eng):
             c = slice(1536 * h, 1536 * h + 1536)
-            nc.sync.dma_start(out=zt[e][:, c], in_=z_v[e][:, c])
-            nc.sync.dma_start(out=gt[e][:, c], in_=g_v[e][:, c])
+            eng.dma_start(out=zt[e][:, c], in_=z_v[e][:, c])
+            eng.dma_start(out=gt[e][:, c], in_=g_v[e][:, c])
 
-        def load_a(e):
+        def load_a(e, eng):
             a = sb.tile([P, 3072], F32, name="a", tag="a", bufs=2)
-            nc.sync.dma_start(out=a[:], in_=a_v[e])
+            eng.dma_start(out=a[:], in_=a_v[e])
             at[e] = a
 
-        def load_w(i, view):
-            wr = sb.tile([P, 4, 1536], BF16, name="wr", tag="wr", bufs=1)
-            nc.sync.dma_start(out=wr[:], in_=view)
+        def load_w(i, view, eng):
+            wr = sb.tile([P, 4, 1536], BF16, name="wr", tag="wr", bufs=2)
+            eng.dma_start(out=wr[:], in_=view)
             wraw[i] = wr
 
         def copy_x(w, s, copy):
             copy(out=xin[w][:, s, 0 : 2 * NI, :].rearrange("p (k i) j -> p i k j", k=2),
                  in_=xraw[w][:].rearrange("p j (i c) -> p i c j", c=12)[:, :, 2 * s : 2 * s + 2, :])
+
+        def copy_pair(w, g, copy):
+            ss = slice(2 * g, 2 * g + 2)
+            copy(out=xin[w][:, ss, 0 : 2 * NI, :].rearrange("p s (k i) j -> p i s k j", k=2),
+                 in_=xraw[w][:].rearrange("p j (i s k) -> p i s k j", s=NP, k=2)[:, :, ss, :, :])
 
         def copy_d(w, g, copy):
             ss = slice(2 * g, 2 * g + 2)
@@ -155,11 +159,11 @@ def tile_dijetresnetblock_pa_v_kernel(tc, x, d_h1, d1, W2, b2, W3, b3, a2, z3, g
             nc.sync.dma_start(out=xscales[64:128, w, :, 0:256].bitcast(I32), in_=tscales[0:64, w, :, :].bitcast(I32))
 
         def keep_odd(w):
-            nc.sync.dma_start(out=xcodes[64:128, w, :, 256:512], in_=tmpc[w][64:128, :, :])
-            nc.sync.dma_start(out=xscales[64:128, w, :, 256:512].bitcast(I32), in_=tscales[64:128, w, :, :].bitcast(I32))
+            nc.vector.tensor_copy(out=xcodes[64:128, w, :, 256:512], in_=tmpc[w][64:128, :, :])
+            nc.vector.tensor_copy(out=xscales[64:128, w, :, 256:512].bitcast(I32), in_=tscales[64:128, w, :, :].bitcast(I32))
 
         def open_w(i):
-            win = sb.tile([P, 512, 4], BF16, name="win", tag="win", bufs=1, align_bytes=64)
+            win = sb.tile([P, 512, 4], BF16, name="win", tag="k4", bufs=2, align_bytes=64)
             wins[i] = win
 
         def prep_w(i, h, copy):
@@ -177,9 +181,9 @@ def tile_dijetresnetblock_pa_v_kernel(tc, x, d_h1, d1, W2, b2, W3, b3, a2, z3, g
             w = sb.tile([P, NP, 512], BF16, name="dz", tag="b6", bufs=5)
             store[e] = w
 
-        def mask2(e, g, h):
+        def mask2(e, g, h=None):
             ss = slice(2 * g, 2 * g + 2)
-            c = slice(256 * h, 256 * h + 256)
+            c = slice(0, 512) if h is None else slice(256 * h, 256 * h + 256)
             nc.vector.scalar_tensor_tensor(out=dz2w[e][:, ss, c].rearrange("q s j -> q j s"), in0=zt[e][:].rearrange("q (j s) -> q j s", s=NP)[:, c, ss],
                                            scalar=0.0, in1=gt[e][:].rearrange("q (j s) -> q j s", s=NP)[:, c, ss], op0=ALU.is_gt, op1=ALU.mult)
 
@@ -201,7 +205,7 @@ def tile_dijetresnetblock_pa_v_kernel(tc, x, d_h1, d1, W2, b2, W3, b3, a2, z3, g
             banks[e, g] = bank
 
         def out2(e, g, copy):
-            ti = sb.tile([P, 256, 4], BF16, name="ti", tag="ti", bufs=3, align_bytes=64)
+            ti = sb.tile([P, 256, 4], BF16, name="ti", tag="ti", bufs=2, align_bytes=64)
             dst = ti[:].rearrange("p c t -> p (c t)").bitcast(F32).rearrange("p (h q u) -> p h q u", h=2, u=2)
             copy(out=dst, in_=banks[e, g][:].rearrange("p h u q -> p h q u"))
             tins[e, g] = ti
@@ -237,13 +241,19 @@ def tile_dijetresnetblock_pa_v_kernel(tc, x, d_h1, d1, W2, b2, W3, b3, a2, z3, g
 
         def outk(g, u, copy):
             if u == 0:
-                ki = sb.tile([P, 512, 4], BF16, name="ki", tag="ki", bufs=2, align_bytes=64)
+                ki = sb.tile([P, 512, 4], BF16, name="ki", tag="k4", bufs=2, align_bytes=64)
                 kins[g] = ki
             dst = kins[g][:].rearrange("m (p u e) t -> m u p e t", u=2, e=2)
             copy(out=dst[:, u], in_=banks["k", g, u][:].rearrange("m t p -> m (t p)").bitcast(BF16).rearrange("m (t p e) -> m p e t", t=4, e=2))
 
+        def open_tok():
+            tcodes = sb.tile([P, G, 512], I32, name="tcodes", tag="c6", align_bytes=64)
+            tkscales = sb.tile([P, G, 512], U8, name="tkscales", tag="s6", align_bytes=64)
+            tok["c"] = tcodes
+            tok["s"] = tkscales
+
         def quantk(g):
-            nc.vector.quantize_mx(out=tcodes[:, g, :].bitcast(E5M2), scales=tkscales[:, g, :], in_=kins[g][:].rearrange("p c t -> p (c t)"))
+            nc.vector.quantize_mx(out=tok["c"][:, g, :].bitcast(E5M2), scales=tok["s"][:, g, :], in_=kins[g][:].rearrange("p c t -> p (c t)"))
 
         def dd(e, s):
             g, half = s // 2, s % 2
@@ -254,19 +264,19 @@ def tile_dijetresnetblock_pa_v_kernel(tc, x, d_h1, d1, W2, b2, W3, b3, a2, z3, g
             accs["d", e, s] = acc
 
         def open_stage(e):
-            st = sb.tile([P, NP, 512], F32, name="st", tag="z", bufs=2)
+            st = sb.tile([P, 128, NP, 4], F32, name="st", tag="z", bufs=2)
             stage[e] = st
 
         def outd(e, s, copy):
-            copy(out=stage[e][:, s, :], in_=accs["d", e, s][:])
+            copy(out=stage[e][:, :, s, :], in_=accs["d", e, s][:].rearrange("q (n i) -> q n i", i=4))
 
         def finish0(e, h):
             o = sb.tile([P, 1536], F32, name="o0", tag="b6", bufs=5)
-            nc.vector.tensor_copy(out=o[:].rearrange("q (i s) -> q i s", s=NP), in_=stage[e][:, :, 256 * h : 256 * h + 256].rearrange("q s i -> q i s"))
+            nc.vector.tensor_copy(out=o[:].rearrange("q (n m i s) -> q n m s i", m=2, i=2, s=NP), in_=stage[e][:, 64 * h : 64 * h + 64].rearrange("q n s (m i) -> q n m s i", m=2))
             stage["o", e, h] = o
 
-        def store0(e, h):
-            nc.sync.dma_start(out=out0_v[e][:, 1536 * h : 1536 * h + 1536], in_=stage["o", e, h][:])
+        def store0(e, h, eng):
+            eng.dma_start(out=out0_v[e][:, 1536 * h : 1536 * h + 1536], in_=stage["o", e, h][:])
 
         def open_rows():
             for i in range(2):
@@ -278,7 +288,7 @@ def tile_dijetresnetblock_pa_v_kernel(tc, x, d_h1, d1, W2, b2, W3, b3, a2, z3, g
             acc = ps.tile([P, 512], F32, name="mm", tag="mm", bufs=5)
             ocols = slice(128 * ot, 128 * ot + 128)
             for g in range(G):
-                nc.tensor.matmul_mx(out=acc[:], lhsT=tcodes[:, g, ocols].bitcast(E5M2), lhsT_scale=tkscales[:, g, ocols],
+                nc.tensor.matmul_mx(out=acc[:], lhsT=tok["c"][:, g, ocols].bitcast(E5M2), lhsT_scale=tok["s"][:, g, ocols],
                                     rhs=xcodes[:, w, g, :].bitcast(E4M3), rhs_scale=xscales[:, w, g, :], start=(g == 0), stop=(g == G - 1))
             accs["w", w, ot] = acc
 
@@ -288,275 +298,267 @@ def tile_dijetresnetblock_pa_v_kernel(tc, x, d_h1, d1, W2, b2, W3, b3, a2, z3, g
             copy(out=r[:, :, 255 * w : 255 * w + 255].rearrange("m h (i k) -> m h i k", k=3), in_=bank[:, :, 0:255].rearrange("m h (k i) -> m h i k", k=3))
             copy(out=r[:, :, 765 + w], in_=bank[:, :, 255])
 
-        def storew(ot, lo, hi):
+        def storew(ot, lo, hi, eng):
             r = rows1[ot]
-            nc.sync.dma_start(out=out1_v[128 * ot : 128 * ot + 128, :, lo:hi], in_=r[:, :, lo:hi])
+            eng.dma_start(out=out1_v[128 * ot : 128 * ot + 128, :, lo:hi], in_=r[:, :, lo:hi])
 
         with tc.manual_schedule():
             warm = sb.tile([P, 1], F32, name="warm")
             nc.vector.memset(warm[:], 0.0)
-            A(out=warm[:], in_=warm[:])
+            nc.scalar.activation(out=warm[:], in_=warm[:], func=mybir.ActivationFunctionType.Sign)
             open_zg(0)
-            load_zg(0, 1)
-            load_zg(0, 0)
-            load_w(3, w3_v)
-            open_dz(dz2w, 0)
-            mask2(0, 2, 1)
-            mask2(0, 0, 1)
-            mask2(0, 1, 1)
-            mask2(0, 1, 0)
-            load_a(0)
-            mask2(0, 0, 0)
-            turn(dz2w, 0, 1)
-            mask2(0, 2, 0)
-            turn(dz2w, 0, 0)
-            out2(0, 1, V)
-            turn(dz2w, 0, 2)
-            quant2(0, 1)
-            out2(0, 0, A)
-            open_w(3)
-            prep_w(3, 0, V)
-            prep_w(3, 1, A)
             open_zg(1)
-            load_zg(1, 1)
-            quant2(0, 0)
-            out2(0, 2, V)
-            quant_w(3)
-            quant2(0, 2)
-            dh(0, 2)
-            dh(0, 1)
-            load_d(0, nc.sync)
-            load_d(1, nc.scalar)
-            dh(0, 3)
-            open_dz(m1, 0)
-            sign1(0, 1, False)
-            dh(0, 0)
-            dh(0, 5)
-            sign1(0, 0, False)
-            sign1(0, 2, False)
-            open_dz(dz1w, 0)
-            mask1(0, 2)
-            mask1(0, 1)
-            dh(0, 4)
-            load_zg(1, 0)
-            mask1(0, 5)
-            mask1(0, 4)
+            load_zg(0, 0, nc.sync)
+            open_dz(dz2w, 0)
             open_dz(dz2w, 1)
-            mask2(1, 2, 1)
-            turn(dz1w, 0, 2)
-            mask1(0, 3)
-            mask1(0, 0)
-            out1(0, 2, A)
-            turn(dz1w, 0, 1)
-            load_a(1)
-            mask2(1, 0, 1)
-            turn(dz1w, 0, 0)
+            mask2(0, 0, 0)
+            load_zg(0, 1, nc.sync)
+            mask2(0, 2, 1)
+            mask2(0, 2, 0)
+            load_zg(1, 0, nc.sync)
+            mask2(0, 0, 1)
+            mask2(0, 1, 0)
+            mask2(1, 1, 0)
+            turn(dz2w, 0, 0)
+            mask2(0, 1, 1)
+            load_zg(1, 1, nc.sync)
+            turn(dz2w, 0, 2)
+            turn(dz2w, 0, 1)
+            out2(0, 0, A)
+            mask2(1, 0, 0)
             mask2(1, 1, 1)
-            out1(0, 1, A)
-            open_xi(0)
-            copy_d(0, 2, V)
-            copy_d(0, 0, A)
-            copy_d(0, 1, V)
-            quant1(0, 2)
-            out1(0, 0, A)
-            open_xi(1)
-            copy_d(1, 2, A)
-            quant1(0, 0)
-            quant1(0, 1)
+            quant2(0, 0)
+            out2(0, 1, A)
+            mask2(1, 2, 1)
+            out2(0, 2, A)
+            quant2(0, 1)
+            mask2(1, 2, 0)
+            mask2(1, 0, 1)
+            load_w(3, w3_v, nc.sync)
+            turn(dz2w, 1, 1)
+            out2(1, 1, A)
+            open_w(3)
+            prep_w(3, 0, A)
+            turn(dz2w, 1, 2)
+            load_a(0, nc.sync)
+            turn(dz2w, 1, 0)
+            load_a(1, nc.sync)
+            quant2(0, 2)
+            out2(1, 2, A)
+            quant2(1, 1)
+            open_dz(m1, 0)
+            open_dz(dz1w, 0)
+            sign1(0, 2, True)
+            load_d(1, nc.scalar)
+            prep_w(3, 1, V)
+            load_d(0, nc.sync)
+            sign1(0, 1, True)
+            out2(1, 0, V)
+            quant_w(3)
+            dh(0, 1)
+            quant2(1, 2)
+            sign1(0, 0, False)
+            quant2(1, 0)
+            mask1(0, 1)
+            dh(0, 0)
             open_x(0)
             load_x(0, 0, nc.sync)
-            load_x(0, 1, nc.scalar)
             load_last(0, nc.sync)
+            mask1(0, 0)
+            dh(0, 5)
+            load_w(2, w2_v, nc.sync)
+            dh(0, 2)
+            dh(0, 4)
+            dh(0, 3)
+            mask1(0, 5)
+            dh(1, 2)
+            turn(dz1w, 0, 0)
+            dh(1, 4)
+            mask1(0, 4)
+            load_x(0, 1, nc.scalar)
+            mask1(0, 2)
+            open_dz(m1, 1)
+            open_dz(dz1w, 1)
+            sign1(1, 2, False)
+            dh(1, 3)
+            mask1(0, 3)
+            turn(dz1w, 0, 2)
+            mask1(1, 4)
+            sign1(1, 1, True)
+            turn(dz1w, 0, 1)
+            out1(0, 0, A)
+            sign1(1, 0, True)
+            quant1(0, 0)
+            out1(0, 2, A)
+            out1(0, 1, A)
+            mask1(1, 3)
+            mask1(1, 2)
+            dh(1, 1)
             load_last(1, nc.scalar)
-            mask2(1, 1, 0)
+            dh(1, 0)
+            dh(1, 5)
+            mask1(1, 1)
+            mask1(1, 0)
+            open_xi(0)
+            copy_d(0, 2, A)
+            quant1(0, 1)
+            copy_d(0, 0, A)
+            turn(dz1w, 1, 0)
+            open_xi(1)
             copy_d(1, 0, A)
-            mask2(1, 0, 0)
-            turn(dz2w, 1, 1)
-            copy_d(1, 1, A)
-            mask2(1, 2, 0)
-            turn(dz2w, 1, 0)
-            out2(1, 1, V)
+            mask1(1, 5)
+            turn(dz1w, 1, 1)
+            copy_d(1, 1, V)
+            copy_d(1, 2, V)
+            quant1(0, 2)
+            out1(1, 0, A)
             open_x(1)
             load_x(1, 0, nc.sync)
-            load_x(1, 1, nc.scalar)
-            turn(dz2w, 1, 2)
-            quant2(1, 1)
-            out2(1, 0, A)
-            open_dz(m1, 1)
-            sign1(1, 1, False)
-            sign1(1, 0, True)
-            dh(1, 2)
-            quant2(1, 0)
-            dh(1, 3)
-            open_dz(dz1w, 1)
-            mask1(1, 2)
-            dh(1, 0)
-            out2(1, 2, A)
-            load_w(2, w2_v)
-            mask1(1, 3)
-            dh(1, 1)
-            sign1(1, 2, True)
-            mask1(1, 0)
-            turn(dz1w, 1, 1)
-            mask1(1, 1)
-            copy_x(0, 2, A)
-            copy_x(0, 3, V)
-            turn(dz1w, 1, 0)
-            quant2(1, 2)
-            out1(1, 1, A)
-            copy_x(0, 1, V)
-            dh(1, 4)
-            copy_last(1, A)
-            copy_x(0, 4, A)
-            dh(1, 5)
-            copy_x(1, 2, V)
-            mask1(1, 5)
-            out1(1, 0, A)
-            mask1(1, 4)
-            copy_x(1, 5, A)
+            copy_last(0, V)
             back(0, 0)
-            copy_x(1, 0, V)
-            copy_last(0, A)
-            quant_x(1, 2)
-            copy_x(1, 1, A)
-            copy_x(1, 3, V)
-            turn(dz1w, 1, 2)
-            copy_x(1, 4, V)
-            outk(0, 0, A)
-            open_tmp(1)
-            quant_x(1, 3)
-            back(0, 1)
-            quant_x(1, 1)
-            quant_x(1, 5)
-            quant_x(1, 4)
-            out1(1, 2, A)
-            keep_odd(1)
-            quant_x(1, 0)
-            back(1, 0)
-            outk(0, 1, A)
-            copy_x(0, 0, V)
-            swap_even(1)
-            copy_x(0, 5, V)
+            copy_pair(0, 2, V)
+            copy_pair(0, 0, V)
+            copy_pair(0, 1, V)
+            load_x(1, 1, nc.scalar)
             open_x(2)
-            load_x(2, 0, nc.sync)
             load_x(2, 1, nc.scalar)
+            out1(1, 1, A)
+            copy_d(0, 1, A)
+            load_x(2, 0, nc.sync)
+            outk(0, 0, A)
+            quant_x(0, 0)
+            copy_last(1, V)
+            open_tmp(0)
+            quant_x(0, 3)
+            back(0, 1)
+            turn(dz1w, 1, 2)
+            quant_x(0, 1)
             open_w(2)
             prep_w(2, 1, V)
-            back(1, 1)
-            outk(1, 0, A)
-            open_tmp(0)
-            quant_x(0, 5)
-            quant_x(0, 3)
-            quant_x(0, 0)
-            prep_w(2, 0, A)
             quant_x(0, 2)
-            back(2, 0)
-            quantk(0)
-            swap_odd(1)
             quant_x(0, 4)
-            outk(1, 1, A)
-            quant_x(0, 1)
-            back(2, 1)
-            swap_even(0)
+            prep_w(2, 0, A)
+            quant_x(0, 5)
+            out1(1, 2, A)
+            back(1, 0)
+            outk(0, 1, A)
             quant_w(2)
-            keep_odd(0)
-            open_xi(2)
-            copy_d(2, 0, V)
-            outk(2, 0, A)
-            dd(0, 1)
-            copy_d(2, 2, V)
-            dd(0, 4)
-            quantk(1)
-            dd(0, 3)
-            copy_last(2, A)
-            copy_d(2, 1, V)
-            outk(2, 1, A)
-            dd(0, 0)
-            copy_x(2, 2, V)
-            swap_odd(0)
-            dd(0, 5)
-            copy_x(2, 0, V)
-            open_stage(0)
-            outd(0, 1, A)
-            quantk(2)
-            outd(0, 4, A)
-            dd(0, 2)
-            quant_x(2, 0)
-            quant_x(2, 2)
-            outd(0, 0, A)
-            dw(1, 2)
-            copy_x(2, 4, V)
-            outd(0, 3, A)
-            copy_x(2, 1, V)
-            quant_x(2, 4)
-            outd(0, 5, A)
-            open_tmp(2)
-            quant_x(2, 1)
-            dw(1, 1)
-            swap_even(2)
-            open_rows()
-            outw(1, 2, V)
-            outd(0, 2, A)
-            copy_x(2, 3, V)
-            dw(1, 0)
-            outw(1, 1, A)
-            copy_x(2, 5, V)
-            quant_x(2, 3)
-            storew(2, 256, 504)
-            dw(0, 3)
-            quant_x(2, 5)
-            outw(1, 0, A)
-            storew(1, 256, 504)
-            finish0(0, 1)
-            keep_odd(2)
-            dw(0, 2)
-            swap_odd(2)
-            outw(0, 3, A)
-            storew(0, 256, 504)
-            dw(0, 0)
-            storew(3, 0, 248)
-            outw(0, 2, A)
-            quant1(1, 1)
+            copy_pair(1, 2, V)
+            copy_pair(1, 1, V)
+            copy_pair(1, 0, A)
+            open_tmp(1)
+            quant_x(1, 5)
             quant1(1, 2)
+            dd(0, 5)
+            dd(0, 3)
+            dd(0, 2)
+            quant_x(1, 2)
+            quant_x(1, 4)
+            quant_x(1, 0)
+            open_xi(2)
+            copy_d(2, 2, V)
+            open_tok()
+            quantk(0)
             quant1(1, 0)
-            dw(0, 1)
-            outw(0, 0, A)
-            finish0(0, 0)
-            store0(0, 1)
-            dd(1, 4)
-            outw(0, 1, A)
+            open_stage(0)
+            outd(0, 5, A)
+            dd(0, 4)
+            outd(0, 4, A)
+            copy_d(2, 1, V)
+            copy_pair(2, 1, A)
+            dd(0, 0)
+            copy_pair(2, 0, V)
+            dd(0, 1)
+            swap_even(0)
+            copy_last(2, A)
+            outk(1, 0, A)
+            copy_d(2, 0, V)
+            quant_x(1, 1)
+            quant_x(1, 3)
+            copy_pair(2, 2, V)
+            swap_even(1)
+            outd(0, 1, A)
+            outd(0, 2, A)
+            quant1(1, 1)
+            swap_odd(0)
+            swap_odd(1)
+            quant_x(2, 4)
+            back(1, 1)
+            outd(0, 0, A)
+            back(2, 0)
+            outd(0, 3, A)
+            back(2, 1)
+            quant_x(2, 2)
+            quant_x(2, 0)
+            outk(1, 1, A)
+            outk(2, 0, A)
             dd(1, 0)
-            open_stage(1)
-            outd(1, 4, V)
+            finish0(0, 0)
             dd(1, 2)
-            storew(1, 0, 256)
-            dd(1, 1)
-            outd(1, 0, V)
-            outd(1, 2, A)
-            store0(0, 0)
             dd(1, 3)
-            outd(1, 1, V)
+            keep_odd(1)
+            keep_odd(0)
+            finish0(0, 1)
+            outk(2, 1, A)
+            quantk(1)
+            open_stage(1)
+            outd(1, 0, A)
+            dd(1, 1)
             dd(1, 5)
-            outd(1, 3, A)
-            dw(2, 1)
-            outd(1, 5, V)
-            storew(2, 0, 256)
-            finish0(1, 0)
-            dw(2, 0)
-            storew(0, 0, 256)
-            outw(2, 1, A)
-            storew(1, 504, 768)
-            dw(2, 2)
-            outw(2, 0, A)
-            finish0(1, 1)
-            store0(1, 0)
-            dw(2, 3)
-            outw(2, 2, A)
+            quantk(2)
+            outd(1, 2, A)
+            dd(1, 4)
             dw(1, 3)
-            outw(2, 3, A)
-            store0(1, 1)
-            outw(1, 3, V)
-            storew(2, 504, 768)
-            storew(0, 504, 768)
-            storew(3, 248, 504)
-            storew(3, 504, 768)
+            open_tmp(2)
+            quant_x(2, 5)
+            quant_x(2, 1)
+            swap_even(2)
+            outd(1, 3, A)
+            dw(0, 1)
+            store0(0, 0, nc.sync)
+            outd(1, 1, A)
+            quant_x(2, 3)
+            open_rows()
+            outw(1, 3, A)
+            store0(0, 1, nc.sync)
+            swap_odd(2)
+            outd(1, 4, V)
+            outd(1, 5, V)
+            dw(0, 3)
+            finish0(1, 0)
+            keep_odd(2)
+            finish0(1, 1)
+            outw(0, 3, V)
+            dw(0, 0)
+            storew(3, 256, 504, nc.scalar)
+            outw(0, 0, V)
+            dw(1, 0)
+            dw(1, 1)
+            outw(0, 1, A)
+            dw(2, 1)
+            outw(1, 0, V)
+            storew(1, 0, 248, nc.scalar)
+            outw(1, 1, V)
+            dw(2, 0)
+            store0(1, 0, nc.sync)
+            dw(0, 2)
+            dw(1, 2)
+            outw(2, 0, V)
+            outw(2, 1, A)
+            storew(1, 248, 504, nc.scalar)
+            store0(1, 1, nc.sync)
+            storew(0, 0, 248, nc.scalar)
+            storew(3, 0, 256, nc.scalar)
+            outw(0, 2, V)
+            dw(2, 2)
+            storew(1, 504, 768, nc.scalar)
+            storew(0, 504, 768, nc.scalar)
+            outw(1, 2, V)
+            outw(2, 2, V)
+            storew(2, 256, 504, nc.scalar)
+            dw(2, 3)
+            outw(2, 3, V)
+            storew(3, 504, 768, nc.scalar)
+            storew(2, 0, 256, nc.scalar)
+            storew(0, 248, 504, nc.sync)
+            storew(2, 504, 768, nc.sync)

@@ -308,257 +308,257 @@ def tile_dijetresnetblock_pa_v_kernel(tc, x, d_h1, d1, W2, b2, W3, b3, a2, z3, g
             nc.scalar.activation(out=warm[:], in_=warm[:], func=mybir.ActivationFunctionType.Sign)
             open_zg(0)
             open_zg(1)
+            load_zg(0, 1, nc.sync)
             load_zg(0, 0, nc.sync)
             open_dz(dz2w, 0)
             open_dz(dz2w, 1)
-            mask2(0, 0, 0)
-            load_zg(0, 1, nc.sync)
-            mask2(0, 2, 1)
-            mask2(0, 2, 0)
-            load_zg(1, 0, nc.sync)
-            mask2(0, 0, 1)
             mask2(0, 1, 0)
-            mask2(1, 1, 0)
-            turn(dz2w, 0, 0)
-            mask2(0, 1, 1)
+            mask2(0, 2, 1)
+            mask2(0, 0, 1)
             load_zg(1, 1, nc.sync)
+            load_zg(1, 0, nc.sync)
+            load_w(3, w3_v, nc.sync)
+            mask2(0, 1, 1)
+            mask2(0, 0, 0)
+            turn(dz2w, 0, 0)
+            mask2(0, 2, 0)
             turn(dz2w, 0, 2)
             turn(dz2w, 0, 1)
-            out2(0, 0, A)
-            mask2(1, 0, 0)
-            mask2(1, 1, 1)
-            quant2(0, 0)
-            out2(0, 1, A)
+            out2(0, 0, V)
             mask2(1, 2, 1)
-            out2(0, 2, A)
-            quant2(0, 1)
-            mask2(1, 2, 0)
             mask2(1, 0, 1)
-            load_w(3, w3_v, nc.sync)
-            turn(dz2w, 1, 1)
-            out2(1, 1, A)
+            out2(0, 2, A)
+            mask2(1, 0, 0)
+            load_a(0, nc.sync)
+            load_last(1, nc.sync)
+            mask2(1, 1, 0)
+            quant2(0, 0)
+            quant2(0, 2)
+            out2(0, 1, A)
+            turn(dz2w, 1, 0)
+            out2(1, 0, A)
+            mask2(1, 1, 1)
+            mask2(1, 2, 0)
+            load_a(1, nc.sync)
             open_w(3)
             prep_w(3, 0, A)
+            quant2(0, 1)
+            quant2(1, 0)
+            turn(dz2w, 1, 1)
             turn(dz2w, 1, 2)
-            load_a(0, nc.sync)
-            turn(dz2w, 1, 0)
-            load_a(1, nc.sync)
-            quant2(0, 2)
+            prep_w(3, 1, V)
             out2(1, 2, A)
-            quant2(1, 1)
+            out2(1, 1, A)
+            quant_w(3)
             open_dz(m1, 0)
             open_dz(dz1w, 0)
-            sign1(0, 2, True)
+            sign1(0, 0, True)
+            quant2(1, 1)
             load_d(1, nc.scalar)
-            prep_w(3, 1, V)
-            load_d(0, nc.sync)
-            sign1(0, 1, True)
-            out2(1, 0, V)
-            quant_w(3)
-            dh(0, 1)
-            quant2(1, 2)
-            sign1(0, 0, False)
-            quant2(1, 0)
-            mask1(0, 1)
-            dh(0, 0)
-            open_x(0)
-            load_x(0, 0, nc.sync)
-            load_last(0, nc.sync)
-            mask1(0, 0)
-            dh(0, 5)
-            load_w(2, w2_v, nc.sync)
+            sign1(0, 2, True)
             dh(0, 2)
-            dh(0, 4)
+            sign1(0, 1, False)
+            quant2(1, 2)
+            dh(0, 1)
             dh(0, 3)
-            mask1(0, 5)
-            dh(1, 2)
-            turn(dz1w, 0, 0)
-            dh(1, 4)
-            mask1(0, 4)
-            load_x(0, 1, nc.scalar)
-            mask1(0, 2)
             open_dz(m1, 1)
             open_dz(dz1w, 1)
-            sign1(1, 2, False)
-            dh(1, 3)
-            mask1(0, 3)
-            turn(dz1w, 0, 2)
-            mask1(1, 4)
-            sign1(1, 1, True)
-            turn(dz1w, 0, 1)
-            out1(0, 0, A)
             sign1(1, 0, True)
-            quant1(0, 0)
-            out1(0, 2, A)
+            mask1(0, 2)
+            load_last(0, nc.sync)
+            mask1(0, 3)
+            dh(0, 5)
+            dh(0, 4)
+            mask1(0, 1)
+            open_x(0)
+            load_x(0, 1, nc.scalar)
+            dh(1, 0)
+            mask1(0, 5)
+            mask1(0, 4)
+            turn(dz1w, 0, 1)
+            dh(0, 0)
+            sign1(1, 2, False)
             out1(0, 1, A)
+            dh(1, 5)
+            dh(1, 1)
+            dh(1, 4)
+            mask1(0, 0)
+            turn(dz1w, 0, 2)
+            mask1(1, 0)
+            mask1(1, 1)
+            turn(dz1w, 0, 0)
+            turn(dz1w, 1, 0)
+            mask1(1, 4)
+            mask1(1, 5)
+            quant1(0, 1)
+            sign1(1, 1, True)
+            out1(0, 2, A)
+            open_x(1)
+            load_x(1, 1, nc.scalar)
+            out1(0, 0, A)
+            dh(1, 3)
+            turn(dz1w, 1, 2)
+            dh(1, 2)
+            quant1(0, 2)
+            load_d(0, nc.sync)
+            out1(1, 0, A)
+            open_xi(0)
+            copy_last(0, A)
+            back(0, 0)
+            load_x(0, 0, nc.sync)
+            open_xi(1)
+            copy_d(1, 2, A)
+            quant1(0, 0)
+            copy_d(0, 0, V)
+            quant1(1, 0)
+            back(0, 1)
+            out1(1, 2, A)
+            copy_d(0, 2, V)
+            copy_d(1, 0, V)
+            load_x(1, 0, nc.sync)
             mask1(1, 3)
             mask1(1, 2)
-            dh(1, 1)
-            load_last(1, nc.scalar)
-            dh(1, 0)
-            dh(1, 5)
-            mask1(1, 1)
-            mask1(1, 0)
-            open_xi(0)
-            copy_d(0, 2, A)
-            quant1(0, 1)
-            copy_d(0, 0, A)
-            turn(dz1w, 1, 0)
-            open_xi(1)
-            copy_d(1, 0, A)
-            mask1(1, 5)
-            turn(dz1w, 1, 1)
-            copy_d(1, 1, V)
-            copy_d(1, 2, V)
-            quant1(0, 2)
-            out1(1, 0, A)
-            open_x(1)
-            load_x(1, 0, nc.sync)
-            copy_last(0, V)
-            back(0, 0)
-            copy_pair(0, 2, V)
-            copy_pair(0, 0, V)
-            copy_pair(0, 1, V)
-            load_x(1, 1, nc.scalar)
-            open_x(2)
-            load_x(2, 1, nc.scalar)
-            out1(1, 1, A)
             copy_d(0, 1, A)
-            load_x(2, 0, nc.sync)
+            load_w(2, w2_v, nc.sync)
+            copy_pair(0, 0, V)
             outk(0, 0, A)
-            quant_x(0, 0)
-            copy_last(1, V)
-            open_tmp(0)
-            quant_x(0, 3)
-            back(0, 1)
-            turn(dz1w, 1, 2)
-            quant_x(0, 1)
-            open_w(2)
-            prep_w(2, 1, V)
-            quant_x(0, 2)
-            quant_x(0, 4)
-            prep_w(2, 0, A)
-            quant_x(0, 5)
-            out1(1, 2, A)
-            back(1, 0)
+            copy_pair(0, 2, A)
+            copy_pair(0, 1, V)
             outk(0, 1, A)
-            quant_w(2)
+            copy_last(1, A)
+            open_x(2)
+            load_x(2, 0, nc.scalar)
+            open_tmp(0)
+            quant_x(0, 1)
+            turn(dz1w, 1, 1)
+            quant_x(0, 0)
+            quant_x(0, 3)
+            quant_x(0, 2)
+            out1(1, 1, A)
+            quant_x(0, 4)
             copy_pair(1, 2, V)
+            quant_x(0, 5)
+            back(1, 0)
             copy_pair(1, 1, V)
-            copy_pair(1, 0, A)
+            back(1, 1)
+            open_xi(2)
+            copy_last(2, V)
             open_tmp(1)
             quant_x(1, 5)
-            quant1(1, 2)
-            dd(0, 5)
-            dd(0, 3)
-            dd(0, 2)
-            quant_x(1, 2)
+            copy_pair(1, 0, V)
+            copy_d(1, 1, A)
             quant_x(1, 4)
-            quant_x(1, 0)
-            open_xi(2)
-            copy_d(2, 2, V)
             open_tok()
             quantk(0)
-            quant1(1, 0)
-            open_stage(0)
-            outd(0, 5, A)
-            dd(0, 4)
-            outd(0, 4, A)
-            copy_d(2, 1, V)
-            copy_pair(2, 1, A)
-            dd(0, 0)
-            copy_pair(2, 0, V)
-            dd(0, 1)
-            swap_even(0)
-            copy_last(2, A)
-            outk(1, 0, A)
-            copy_d(2, 0, V)
-            quant_x(1, 1)
-            quant_x(1, 3)
-            copy_pair(2, 2, V)
-            swap_even(1)
-            outd(0, 1, A)
-            outd(0, 2, A)
+            load_x(2, 1, nc.sync)
             quant1(1, 1)
-            swap_odd(0)
-            swap_odd(1)
-            quant_x(2, 4)
-            back(1, 1)
-            outd(0, 0, A)
+            open_w(2)
+            prep_w(2, 1, V)
+            quant_x(1, 2)
+            swap_even(0)
+            copy_d(2, 0, A)
+            prep_w(2, 0, A)
+            quant_w(2)
             back(2, 0)
-            outd(0, 3, A)
-            back(2, 1)
-            quant_x(2, 2)
-            quant_x(2, 0)
-            outk(1, 1, A)
+            quant_x(1, 1)
+            copy_d(2, 1, V)
+            copy_d(2, 2, A)
             outk(2, 0, A)
-            dd(1, 0)
+            dd(0, 4)
+            dd(0, 1)
+            copy_pair(2, 1, V)
+            swap_odd(0)
+            quant_x(1, 0)
+            copy_pair(2, 2, V)
+            quant1(1, 2)
+            copy_pair(2, 0, V)
+            quant_x(2, 2)
+            dd(0, 2)
+            swap_even(1)
+            outk(1, 0, A)
+            dd(0, 3)
+            open_stage(0)
+            outd(0, 1, A)
+            dd(0, 5)
+            outd(0, 4, A)
+            dd(0, 0)
+            quant_x(2, 4)
+            quant_x(2, 0)
+            dd(1, 5)
+            outd(0, 3, A)
+            keep_odd(0)
+            outd(0, 2, A)
+            outd(0, 5, A)
+            outd(0, 0, A)
+            dd(1, 1)
+            back(2, 1)
+            finish0(0, 1)
+            outk(1, 1, A)
+            outk(2, 1, A)
+            dd(1, 4)
+            quant_x(1, 3)
+            open_stage(1)
+            outd(1, 5, A)
             finish0(0, 0)
             dd(1, 2)
-            dd(1, 3)
-            keep_odd(1)
-            keep_odd(0)
-            finish0(0, 1)
-            outk(2, 1, A)
+            store0(0, 0, nc.scalar)
             quantk(1)
-            open_stage(1)
-            outd(1, 0, A)
-            dd(1, 1)
-            dd(1, 5)
-            quantk(2)
-            outd(1, 2, A)
-            dd(1, 4)
-            dw(1, 3)
-            open_tmp(2)
-            quant_x(2, 5)
-            quant_x(2, 1)
-            swap_even(2)
-            outd(1, 3, A)
-            dw(0, 1)
-            store0(0, 0, nc.sync)
             outd(1, 1, A)
+            swap_even(2)
+            quantk(2)
+            dd(1, 0)
+            dd(1, 3)
+            outd(1, 4, A)
+            open_tmp(2)
             quant_x(2, 3)
-            open_rows()
-            outw(1, 3, A)
-            store0(0, 1, nc.sync)
-            swap_odd(2)
-            outd(1, 4, V)
-            outd(1, 5, V)
-            dw(0, 3)
-            finish0(1, 0)
-            keep_odd(2)
-            finish0(1, 1)
-            outw(0, 3, V)
-            dw(0, 0)
-            storew(3, 256, 504, nc.scalar)
-            outw(0, 0, V)
-            dw(1, 0)
-            dw(1, 1)
-            outw(0, 1, A)
-            dw(2, 1)
-            outw(1, 0, V)
-            storew(1, 0, 248, nc.scalar)
-            outw(1, 1, V)
-            dw(2, 0)
-            store0(1, 0, nc.sync)
             dw(0, 2)
-            dw(1, 2)
-            outw(2, 0, V)
-            outw(2, 1, A)
-            storew(1, 248, 504, nc.scalar)
+            quant_x(2, 1)
+            quant_x(2, 5)
+            outd(1, 3, A)
+            store0(0, 1, nc.sync)
+            outd(1, 2, V)
+            open_rows()
+            outw(0, 2, A)
+            dw(0, 0)
+            outd(1, 0, V)
+            swap_odd(1)
+            dw(0, 1)
+            storew(2, 0, 248, nc.scalar)
+            swap_odd(2)
+            finish0(1, 1)
+            outw(0, 0, A)
             store0(1, 1, nc.sync)
+            dw(0, 3)
+            keep_odd(1)
             storew(0, 0, 248, nc.scalar)
-            storew(3, 0, 256, nc.scalar)
-            outw(0, 2, V)
-            dw(2, 2)
-            storew(1, 504, 768, nc.scalar)
-            storew(0, 504, 768, nc.scalar)
-            outw(1, 2, V)
-            outw(2, 2, V)
-            storew(2, 256, 504, nc.scalar)
+            dw(1, 2)
+            keep_odd(2)
+            dw(1, 3)
+            outw(0, 1, V)
             dw(2, 3)
+            dw(1, 0)
+            finish0(1, 0)
             outw(2, 3, V)
-            storew(3, 504, 768, nc.scalar)
-            storew(2, 0, 256, nc.scalar)
+            outw(0, 3, A)
+            storew(1, 0, 248, nc.scalar)
+            dw(2, 0)
+            outw(1, 2, A)
+            storew(2, 248, 504, nc.scalar)
+            outw(2, 0, V)
+            outw(1, 3, A)
+            dw(2, 2)
+            dw(1, 1)
+            store0(1, 0, nc.scalar)
+            dw(2, 1)
+            storew(3, 0, 248, nc.sync)
+            storew(3, 248, 504, nc.scalar)
+            storew(3, 504, 768, nc.sync)
+            outw(2, 2, V)
+            outw(1, 0, A)
+            outw(1, 1, A)
+            storew(1, 248, 504, nc.scalar)
+            storew(0, 504, 768, nc.sync)
             storew(0, 248, 504, nc.sync)
+            outw(2, 1, A)
             storew(2, 504, 768, nc.sync)
+            storew(1, 504, 768, nc.scalar)

from contextlib import ExitStack

import concourse.mybir as mybir
from concourse.masks import make_identity

F32 = mybir.dt.float32
BF16 = mybir.dt.bfloat16
I32 = mybir.dt.int32
U8 = mybir.dt.uint8
E4M3 = mybir.dt.float8_e4m3fn_x4
E5M2 = mybir.dt.float8_e5m2_x4
ALU = mybir.AluOpType

P = 128
N, ND, NP, KW = 256, 512, 6, 3
T = N * NP
FLOPS = 2 * (2 * T * ND * ND + T * KW * ND * ND)
BYTES = 2 * (N * ND * 12 + N * ND * 6 * 2 + 2 * ND * ND) + 4 * (2 * N * ND * 6) + 4 * (N * ND * 6 + ND * ND * 3)

G = 3
NI = 85


def tile_dijetresnetblock_pa_v_kernel(tc, x, d_h1, d1, W2, b2, W3, b3, a2, z3, grad_out, out_0, out_1):
    nc = tc.nc

    x_v = x.rearrange("(p j) (h c) s -> h p j (c s)", j=4, h=2)
    d_v = d_h1.rearrange("(p j) (h c) s -> h p j (c s)", j=4, h=2)
    z_v = z3.rearrange("(q e) c s -> e q (c s)", e=2)
    a_v = a2.rearrange("(q e) c s -> e q (c s)", e=2)
    g_v = grad_out.rearrange("(q e) c s -> e q (c s)", e=2)
    w2_v = W2.rearrange("(p t) i k -> p t (i k)", t=4)
    w3_v = W3.rearrange("(p t) i k -> p t (i k)", t=4)
    out0_v = out_0.rearrange("(q e) c s -> e q (c s)", e=2)
    out1_v = out_1.rearrange("o (h c) k -> o h (c k)", h=2)
    V = nc.vector.tensor_copy
    A = nc.scalar.copy

    with ExitStack() as ctx:
        sb = ctx.enter_context(tc.tile_pool(name="sb", bufs=1))
        ps = ctx.enter_context(tc.psum_pool(name="ps", bufs=1))

        ident = sb.tile([P, P], F32, name="ident")
        make_identity(nc, ident[:])

        xcodes = sb.tile([P, 3, G, 512], I32, name="xcodes", align_bytes=64)
        xscales = sb.tile([P, 3, G, 512], U8, name="xscales", align_bytes=64)
        nc.gpsimd.memset(xscales[:].rearrange("p a b c -> p (a b c)").bitcast(I32), 0)
        tscales = sb.tile([P, 3, G, 256], U8, name="tscales", align_bytes=64)
        nc.gpsimd.memset(tscales[:].rearrange("p a b c -> p (a b c)").bitcast(I32), 0)
        codes2 = sb.tile([P, 2, G, 256], I32, name="codes2", tag="c6", align_bytes=64)
        scales2 = sb.tile([P, 2, G, 256], U8, name="scales2", tag="s6", align_bytes=64)
        dz1t = sb.tile([P, G, 2, 256, 4], BF16, name="dz1t", align_bytes=64)
        codes1 = sb.tile([P, G, 2, 256], I32, name="codes1", align_bytes=64)
        scales1 = sb.tile([P, G, 2, 256], U8, name="scales1", align_bytes=64)
        tok = {}
        draw = sb.tile([P, 4, 256 * 6], BF16, name="draw")
        xlast = sb.tile([P, 4, 12], BF16, name="xlast")

        xraw = {}
        xin = {}
        tmpc = {}
        zt = {}
        gt = {}
        at = {}
        wraw = {}
        wins = {}
        wcodes = {}
        wscales = {}
        dz2w = {}
        dz1w = {}
        m1 = {}
        stage = {}
        rows1 = {}
        banks = {}
        tins = {}
        accs = {}
        kins = {}

        def open_x(w):
            xr = sb.tile([P, 4, NI * 12], BF16, name="xr", tag="xr", bufs=3)
            xraw[w] = xr

        def open_xi(w):
            xi = sb.tile([P, NP, 256, 4], BF16, name="xi", tag="xi", bufs=2, align_bytes=64)
            xin[w] = xi

        def open_tmp(w):
            tm = sb.tile([P, G, 256], I32, name="tm", tag="tm", bufs=2, align_bytes=64)
            tmpc[w] = tm

        def load_x(w, h, eng):
            eng.dma_start(out=xraw[w][64 * h : 64 * h + 64], in_=x_v[h][:, :, 12 * NI * w : 12 * NI * (w + 1)])

        def load_last(h, eng):
            eng.dma_start(out=xlast[64 * h : 64 * h + 64], in_=x_v[h][:, :, 12 * 255 : 12 * 256])

        def load_d(h, eng):
            eng.dma_start(out=draw[64 * h : 64 * h + 64], in_=d_v[h])

        def open_zg(e):
            z = sb.tile([P, 3072], F32, name="z", tag="z", bufs=2)
            g = sb.tile([P, 3072], BF16, name="g", tag="b6", bufs=5)
            zt[e] = z
            gt[e] = g

        def load_zg(e, h, eng):
            c = slice(1536 * h, 1536 * h + 1536)
            eng.dma_start(out=zt[e][:, c], in_=z_v[e][:, c])
            eng.dma_start(out=gt[e][:, c], in_=g_v[e][:, c])

        def load_a(e, eng):
            a = sb.tile([P, 3072], F32, name="a", tag="a", bufs=2)
            eng.dma_start(out=a[:], in_=a_v[e])
            at[e] = a

        def load_w(i, view, eng):
            wr = sb.tile([P, 4, 1536], BF16, name="wr", tag="wr", bufs=2)
            eng.dma_start(out=wr[:], in_=view)
            wraw[i] = wr

        def copy_x(w, s, copy):
            copy(out=xin[w][:, s, 0 : 2 * NI, :].rearrange("p (k i) j -> p i k j", k=2),
                 in_=xraw[w][:].rearrange("p j (i c) -> p i c j", c=12)[:, :, 2 * s : 2 * s + 2, :])

        def copy_pair(w, g, copy):
            ss = slice(2 * g, 2 * g + 2)
            copy(out=xin[w][:, ss, 0 : 2 * NI, :].rearrange("p s (k i) j -> p i s k j", k=2),
                 in_=xraw[w][:].rearrange("p j (i s k) -> p i s k j", s=NP, k=2)[:, :, ss, :, :])

        def copy_d(w, g, copy):
            ss = slice(2 * g, 2 * g + 2)
            copy(out=xin[w][:, ss, 2 * NI : 3 * NI, :].rearrange("p s i j -> p i s j"),
                 in_=draw[:].rearrange("p j (i c) -> p i c j", c=6)[:, NI * w : NI * (w + 1), ss, :])

        def copy_last(w, copy):
            if w < 2:
                src = xlast[:].rearrange("p j (s k) -> p s k j", k=2)[:, :, w, :]
            else:
                src = draw[:].rearrange("p j (i c) -> p i c j", c=6)[:, 255, :, :]
            copy(out=xin[w][:, :, 255, :], in_=src)

        def quant_x(w, s):
            g = s // 2
            if s % 2 == 0:
                out = xcodes[:, w, g, 0:256]
                sc = xscales[:, w, g, 0:256]
            else:
                out = tmpc[w][:, g, :]
                sc = tscales[:, w, g, :]
            nc.vector.quantize_mx(out=out.bitcast(E4M3), scales=sc, in_=xin[w][:, s, :, :].rearrange("p c j -> p (c j)"))

        def swap_even(w):
            nc.sync.dma_start(out=xcodes[0:64, w, :, 256:512], in_=xcodes[64:128, w, :, 0:256])
            nc.sync.dma_start(out=xscales[0:64, w, :, 256:512].bitcast(I32), in_=xscales[64:128, w, :, 0:256].bitcast(I32))

        def swap_odd(w):
            nc.sync.dma_start(out=xcodes[64:128, w, :, 0:256], in_=tmpc[w][0:64, :, :])
            nc.sync.dma_start(out=xscales[64:128, w, :, 0:256].bitcast(I32), in_=tscales[0:64, w, :, :].bitcast(I32))

        def keep_odd(w):
            nc.vector.tensor_copy(out=xcodes[64:128, w, :, 256:512], in_=tmpc[w][64:128, :, :])
            nc.vector.tensor_copy(out=xscales[64:128, w, :, 256:512].bitcast(I32), in_=tscales[64:128, w, :, :].bitcast(I32))

        def open_w(i):
            win = sb.tile([P, 512, 4], BF16, name="win", tag="k4", bufs=2, align_bytes=64)
            wins[i] = win

        def prep_w(i, h, copy):
            c = slice(256 * h, 256 * h + 256)
            copy(out=wins[i][:, c, :], in_=wraw[i][:].rearrange("p t (c k) -> p c k t", k=3)[:, c, 2, :])

        def quant_w(i):
            wc = sb.tile([P, 512], I32, name="wc", tag="wc", bufs=2, align_bytes=64)
            ws = sb.tile([P, 512], U8, name="ws", tag="ws", bufs=2, align_bytes=64)
            nc.vector.quantize_mx(out=wc[:].bitcast(E4M3), scales=ws[:], in_=wins[i][:].rearrange("p c t -> p (c t)"))
            wcodes[i] = wc
            wscales[i] = ws

        def open_dz(store, e):
            w = sb.tile([P, NP, 512], BF16, name="dz", tag="b6", bufs=5)
            store[e] = w

        def mask2(e, g, h=None):
            ss = slice(2 * g, 2 * g + 2)
            c = slice(0, 512) if h is None else slice(256 * h, 256 * h + 256)
            nc.vector.scalar_tensor_tensor(out=dz2w[e][:, ss, c].rearrange("q s j -> q j s"), in0=zt[e][:].rearrange("q (j s) -> q j s", s=NP)[:, c, ss],
                                           scalar=0.0, in1=gt[e][:].rearrange("q (j s) -> q j s", s=NP)[:, c, ss], op0=ALU.is_gt, op1=ALU.mult)

        def sign1(e, g, act):
            ss = slice(2 * g, 2 * g + 2)
            dst = m1[e][:, ss, :].rearrange("q s o -> q o s")
            src = at[e][:].rearrange("q (o s) -> q o s", s=NP)[:, :, ss]
            if act:
                nc.scalar.activation(out=dst, in_=src, func=mybir.ActivationFunctionType.Sign)
            else:
                nc.vector.tensor_scalar(out=dst, in0=src, scalar1=0.0, scalar2=None, op0=ALU.is_gt)

        def turn(src, e, g):
            bank = ps.tile([P, 2, 2, P], F32, name="tp", tag="tp", bufs=3)
            for half in range(2):
                words = src[e][:, 2 * g + half, :].bitcast(F32)
                for u in range(2):
                    nc.tensor.transpose(bank[:, half, u, :], words[:, u:256:2], ident[:])
            banks[e, g] = bank

        def out2(e, g, copy):
            ti = sb.tile([P, 256, 4], BF16, name="ti", tag="ti", bufs=2, align_bytes=64)
            dst = ti[:].rearrange("p c t -> p (c t)").bitcast(F32).rearrange("p (h q u) -> p h q u", h=2, u=2)
            copy(out=dst, in_=banks[e, g][:].rearrange("p h u q -> p h q u"))
            tins[e, g] = ti

        def quant2(e, g):
            nc.vector.quantize_mx(out=codes2[:, e, g, :].bitcast(E5M2), scales=scales2[:, e, g, :], in_=tins[e, g][:].rearrange("p c t -> p (c t)"))

        def dh(e, s):
            g, half = s // 2, s % 2
            acc = ps.tile([P, 512], F32, name="mm", tag="mm", bufs=5)
            cols = slice(128 * half, 128 * half + 128)
            nc.tensor.matmul_mx(out=acc[:], lhsT=codes2[:, e, g, cols].bitcast(E5M2), lhsT_scale=scales2[:, e, g, cols],
                                rhs=wcodes[3][:].bitcast(E4M3), rhs_scale=wscales[3][:], start=True, stop=True)
            accs[e, s] = acc

        def mask1(e, s):
            nc.vector.scalar_tensor_tensor(out=dz1w[e][:, s, :], in0=m1[e][:, s, :], scalar=0.0, in1=accs[e, s][:], op0=ALU.max, op1=ALU.mult)

        def out1(e, g, copy):
            dst = dz1t[:, g, e, :, :].rearrange("p c t -> p (c t)").bitcast(F32).rearrange("p (h q u) -> p h q u", h=2, u=2)
            copy(out=dst, in_=banks[e, g][:].rearrange("p h u q -> p h q u"))

        def quant1(e, g):
            nc.vector.quantize_mx(out=codes1[:, g, e, :].bitcast(E5M2), scales=scales1[:, g, e, :],
                                  in_=dz1t[:, g, e, :, :].rearrange("p c t -> p (c t)"))

        def back(g, u):
            bank = ps.tile([P, 4, P], F32, name="tp", tag="tp", bufs=3)
            for t in range(4):
                words = dz1t[:, g, t % 2, :, :].rearrange("p c t -> p (c t)").bitcast(F32)
                nc.tensor.transpose(bank[:, t, :], words[:, 2 * (t // 2) + u : 512 : 4], ident[:])
            banks["k", g, u] = bank

        def outk(g, u, copy):
            if u == 0:
                ki = sb.tile([P, 512, 4], BF16, name="ki", tag="k4", bufs=2, align_bytes=64)
                kins[g] = ki
            dst = kins[g][:].rearrange("m (p u e) t -> m u p e t", u=2, e=2)
            copy(out=dst[:, u], in_=banks["k", g, u][:].rearrange("m t p -> m (t p)").bitcast(BF16).rearrange("m (t p e) -> m p e t", t=4, e=2))

        def open_tok():
            tcodes = sb.tile([P, G, 512], I32, name="tcodes", tag="c6", align_bytes=64)
            tkscales = sb.tile([P, G, 512], U8, name="tkscales", tag="s6", align_bytes=64)
            tok["c"] = tcodes
            tok["s"] = tkscales

        def quantk(g):
            nc.vector.quantize_mx(out=tok["c"][:, g, :].bitcast(E5M2), scales=tok["s"][:, g, :], in_=kins[g][:].rearrange("p c t -> p (c t)"))

        def dd(e, s):
            g, half = s // 2, s % 2
            acc = ps.tile([P, 512], F32, name="mm", tag="mm", bufs=5)
            cols = slice(128 * half, 128 * half + 128)
            nc.tensor.matmul_mx(out=acc[:], lhsT=codes1[:, g, e, cols].bitcast(E5M2), lhsT_scale=scales1[:, g, e, cols],
                                rhs=wcodes[2][:].bitcast(E4M3), rhs_scale=wscales[2][:], start=True, stop=True)
            accs["d", e, s] = acc

        def open_stage(e):
            st = sb.tile([P, 128, NP, 4], F32, name="st", tag="z", bufs=2)
            stage[e] = st

        def outd(e, s, copy):
            copy(out=stage[e][:, :, s, :], in_=accs["d", e, s][:].rearrange("q (n i) -> q n i", i=4))

        def finish0(e, h):
            o = sb.tile([P, 1536], F32, name="o0", tag="b6", bufs=5)
            nc.vector.tensor_copy(out=o[:].rearrange("q (n m i s) -> q n m s i", m=2, i=2, s=NP), in_=stage[e][:, 64 * h : 64 * h + 64].rearrange("q n s (m i) -> q n m s i", m=2))
            stage["o", e, h] = o

        def store0(e, h, eng):
            eng.dma_start(out=out0_v[e][:, 1536 * h : 1536 * h + 1536], in_=stage["o", e, h][:])

        def open_rows():
            for i in range(2):
                r = sb.tile([P, 2, 2, 768], F32, name="r1", tag="a", bufs=2)
                rows1[2 * i] = r[:, 0]
                rows1[2 * i + 1] = r[:, 1]

        def dw(w, ot):
            acc = ps.tile([P, 512], F32, name="mm", tag="mm", bufs=5)
            ocols = slice(128 * ot, 128 * ot + 128)
            for g in range(G):
                nc.tensor.matmul_mx(out=acc[:], lhsT=tok["c"][:, g, ocols].bitcast(E5M2), lhsT_scale=tok["s"][:, g, ocols],
                                    rhs=xcodes[:, w, g, :].bitcast(E4M3), rhs_scale=xscales[:, w, g, :], start=(g == 0), stop=(g == G - 1))
            accs["w", w, ot] = acc

        def outw(w, ot, copy):
            r = rows1[ot]
            bank = accs["w", w, ot][:].rearrange("m (h c) -> m h c", h=2)
            copy(out=r[:, :, 255 * w : 255 * w + 255].rearrange("m h (i k) -> m h i k", k=3), in_=bank[:, :, 0:255].rearrange("m h (k i) -> m h i k", k=3))
            copy(out=r[:, :, 765 + w], in_=bank[:, :, 255])

        def storew(ot, lo, hi, eng):
            r = rows1[ot]
            eng.dma_start(out=out1_v[128 * ot : 128 * ot + 128, :, lo:hi], in_=r[:, :, lo:hi])

        with tc.manual_schedule():
            warm = sb.tile([P, 1], F32, name="warm")
            nc.vector.memset(warm[:], 0.0)
            nc.scalar.activation(out=warm[:], in_=warm[:], func=mybir.ActivationFunctionType.Sign)
            open_zg(0)
            open_zg(1)
            load_zg(0, 1, nc.sync)
            load_zg(0, 0, nc.sync)
            open_dz(dz2w, 0)
            open_dz(dz2w, 1)
            mask2(0, 1, 0)
            mask2(0, 2, 1)
            mask2(0, 0, 1)
            load_zg(1, 1, nc.sync)
            load_zg(1, 0, nc.sync)
            load_w(3, w3_v, nc.sync)
            mask2(0, 1, 1)
            mask2(0, 0, 0)
            turn(dz2w, 0, 0)
            mask2(0, 2, 0)
            turn(dz2w, 0, 2)
            turn(dz2w, 0, 1)
            out2(0, 0, V)
            mask2(1, 2, 1)
            mask2(1, 0, 1)
            out2(0, 2, A)
            mask2(1, 0, 0)
            load_a(0, nc.sync)
            load_last(1, nc.sync)
            mask2(1, 1, 0)
            quant2(0, 0)
            quant2(0, 2)
            out2(0, 1, A)
            turn(dz2w, 1, 0)
            out2(1, 0, A)
            mask2(1, 1, 1)
            mask2(1, 2, 0)
            load_a(1, nc.sync)
            open_w(3)
            prep_w(3, 0, A)
            quant2(0, 1)
            quant2(1, 0)
            turn(dz2w, 1, 1)
            turn(dz2w, 1, 2)
            prep_w(3, 1, V)
            out2(1, 2, A)
            out2(1, 1, A)
            quant_w(3)
            open_dz(m1, 0)
            open_dz(dz1w, 0)
            sign1(0, 0, True)
            quant2(1, 1)
            load_d(1, nc.scalar)
            sign1(0, 2, True)
            dh(0, 2)
            sign1(0, 1, False)
            quant2(1, 2)
            dh(0, 1)
            dh(0, 3)
            open_dz(m1, 1)
            open_dz(dz1w, 1)
            sign1(1, 0, True)
            mask1(0, 2)
            load_last(0, nc.sync)
            mask1(0, 3)
            dh(0, 5)
            dh(0, 4)
            mask1(0, 1)
            open_x(0)
            load_x(0, 1, nc.scalar)
            dh(1, 0)
            mask1(0, 5)
            mask1(0, 4)
            turn(dz1w, 0, 1)
            dh(0, 0)
            sign1(1, 2, False)
            out1(0, 1, A)
            dh(1, 5)
            dh(1, 1)
            dh(1, 4)
            mask1(0, 0)
            turn(dz1w, 0, 2)
            mask1(1, 0)
            mask1(1, 1)
            turn(dz1w, 0, 0)
            turn(dz1w, 1, 0)
            mask1(1, 4)
            mask1(1, 5)
            quant1(0, 1)
            sign1(1, 1, True)
            out1(0, 2, A)
            open_x(1)
            load_x(1, 1, nc.scalar)
            out1(0, 0, A)
            dh(1, 3)
            turn(dz1w, 1, 2)
            dh(1, 2)
            quant1(0, 2)
            load_d(0, nc.sync)
            out1(1, 0, A)
            open_xi(0)
            copy_last(0, A)
            back(0, 0)
            load_x(0, 0, nc.sync)
            open_xi(1)
            copy_d(1, 2, A)
            quant1(0, 0)
            copy_d(0, 0, V)
            quant1(1, 0)
            back(0, 1)
            out1(1, 2, A)
            copy_d(0, 2, V)
            copy_d(1, 0, V)
            load_x(1, 0, nc.sync)
            mask1(1, 3)
            mask1(1, 2)
            copy_d(0, 1, A)
            load_w(2, w2_v, nc.sync)
            copy_pair(0, 0, V)
            outk(0, 0, A)
            copy_pair(0, 2, A)
            copy_pair(0, 1, V)
            outk(0, 1, A)
            copy_last(1, A)
            open_x(2)
            load_x(2, 0, nc.scalar)
            open_tmp(0)
            quant_x(0, 1)
            turn(dz1w, 1, 1)
            quant_x(0, 0)
            quant_x(0, 3)
            quant_x(0, 2)
            out1(1, 1, A)
            quant_x(0, 4)
            copy_pair(1, 2, V)
            quant_x(0, 5)
            back(1, 0)
            copy_pair(1, 1, V)
            back(1, 1)
            open_xi(2)
            copy_last(2, V)
            open_tmp(1)
            quant_x(1, 5)
            copy_pair(1, 0, V)
            copy_d(1, 1, A)
            quant_x(1, 4)
            open_tok()
            quantk(0)
            load_x(2, 1, nc.sync)
            quant1(1, 1)
            open_w(2)
            prep_w(2, 1, V)
            quant_x(1, 2)
            swap_even(0)
            copy_d(2, 0, A)
            prep_w(2, 0, A)
            quant_w(2)
            back(2, 0)
            quant_x(1, 1)
            copy_d(2, 1, V)
            copy_d(2, 2, A)
            outk(2, 0, A)
            dd(0, 4)
            dd(0, 1)
            copy_pair(2, 1, V)
            swap_odd(0)
            quant_x(1, 0)
            copy_pair(2, 2, V)
            quant1(1, 2)
            copy_pair(2, 0, V)
            quant_x(2, 2)
            dd(0, 2)
            swap_even(1)
            outk(1, 0, A)
            dd(0, 3)
            open_stage(0)
            outd(0, 1, A)
            dd(0, 5)
            outd(0, 4, A)
            dd(0, 0)
            quant_x(2, 4)
            quant_x(2, 0)
            dd(1, 5)
            outd(0, 3, A)
            keep_odd(0)
            outd(0, 2, A)
            outd(0, 5, A)
            outd(0, 0, A)
            dd(1, 1)
            back(2, 1)
            finish0(0, 1)
            outk(1, 1, A)
            outk(2, 1, A)
            dd(1, 4)
            quant_x(1, 3)
            open_stage(1)
            outd(1, 5, A)
            finish0(0, 0)
            dd(1, 2)
            store0(0, 0, nc.scalar)
            quantk(1)
            outd(1, 1, A)
            swap_even(2)
            quantk(2)
            dd(1, 0)
            dd(1, 3)
            outd(1, 4, A)
            open_tmp(2)
            quant_x(2, 3)
            dw(0, 2)
            quant_x(2, 1)
            quant_x(2, 5)
            outd(1, 3, A)
            store0(0, 1, nc.sync)
            outd(1, 2, V)
            open_rows()
            outw(0, 2, A)
            dw(0, 0)
            outd(1, 0, V)
            swap_odd(1)
            dw(0, 1)
            storew(2, 0, 248, nc.scalar)
            swap_odd(2)
            finish0(1, 1)
            outw(0, 0, A)
            store0(1, 1, nc.sync)
            dw(0, 3)
            keep_odd(1)
            storew(0, 0, 248, nc.scalar)
            dw(1, 2)
            keep_odd(2)
            dw(1, 3)
            outw(0, 1, V)
            dw(2, 3)
            dw(1, 0)
            finish0(1, 0)
            outw(2, 3, V)
            outw(0, 3, A)
            storew(1, 0, 248, nc.scalar)
            dw(2, 0)
            outw(1, 2, A)
            storew(2, 248, 504, nc.scalar)
            outw(2, 0, V)
            outw(1, 3, A)
            dw(2, 2)
            dw(1, 1)
            store0(1, 0, nc.scalar)
            dw(2, 1)
            storew(3, 0, 248, nc.sync)
            storew(3, 248, 504, nc.scalar)
            storew(3, 504, 768, nc.sync)
            outw(2, 2, V)
            outw(1, 0, A)
            outw(1, 1, A)
            storew(1, 248, 504, nc.scalar)
            storew(0, 504, 768, nc.sync)
            storew(0, 248, 504, nc.sync)
            outw(2, 1, A)
            storew(2, 504, 768, nc.sync)
            storew(1, 504, 768, nc.scalar)
